import numpy as np
import ml_dtypes


def mxq(x, axis, fmt="e4m3"):
    dtype, down = {"e4m3": (ml_dtypes.float8_e4m3fn, 7), "e5m2": (ml_dtypes.float8_e5m2, 14)}[fmt]
    v = np.moveaxis(np.asarray(x, np.float32).astype(ml_dtypes.bfloat16).astype(np.float64), axis, -1)
    blocks = v.reshape(v.shape[:-1] + (-1, 32))
    amax = np.abs(blocks).max(-1, keepdims=True)
    byte = np.maximum(np.where(amax > 0, np.frexp(amax)[1] - 1 + 127, 0) - down, 1)
    scale = np.exp2(byte - 127.0)
    codes = (blocks / scale).astype(np.float32).astype(dtype).astype(np.float64)
    return np.moveaxis((codes * scale).reshape(v.shape), -1, axis)


WIDE = False


def mx_kscale(k):
    if not WIDE:
        return np.ones(k)
    levels = np.array([10, -10, 5, -5, 0])
    a = np.random.permutation(np.resize(levels, k // 512 * 4)).reshape(k // 512, 4)
    idx = np.arange(k)
    return np.exp2(a[idx // 512, idx % 128 // 32])


BF16 = ml_dtypes.bfloat16


def bf(x):
    return np.asarray(x, np.float32).astype(BF16)


def f64(x):
    return np.asarray(x).astype(np.float64)


B, C, T, DK, DV, P = 4, 512, 4096, 128, 256, 4


def maxpool(y):
    b, ch, t = y.shape
    return y.reshape(b, ch, t // P, P).max(axis=-1)


def setup_inputs():
    s = mx_kscale(C)
    return {"x": bf(np.random.standard_normal((B, C, T)) * s[:, None]),
            "Wq": bf(np.random.standard_normal((DK, C)) * 0.5 / np.sqrt(C) / s),
            "Wk": bf(np.random.standard_normal((DK, C)) * 0.5 / np.sqrt(C) / s),
            "Wv": bf(np.random.standard_normal((DV, C)) / np.sqrt(C) / s)}


def reference(x, Wq, Wk, Wv):
    xq = mxq(f64(x), 1, "e4m3")
    q = mxq(f64(Wq), 1, "e4m3") @ xq
    k = maxpool(mxq(f64(Wk), 1, "e4m3") @ xq)
    v = maxpool(mxq(f64(Wv), 1, "e4m3") @ xq)
    return q, k, v

@@ -1,0 +1,167 @@
+from contextlib import ExitStack
+
+import concourse.mybir as mybir
+from concourse.masks import make_identity
+
+BF16 = mybir.dt.bfloat16
+F32 = mybir.dt.float32
+U32 = mybir.dt.uint32
+U8 = mybir.dt.uint8
+FP8X4 = mybir.dt.float8_e4m3fn_x4
+
+P = 128
+PACK = 4
+BATCH, CHANNELS, TIME = 4, 512, 4096
+WINDOW = 4
+HEADS = 4
+POOLED_HEADS = HEADS - 1
+UNIT = 512
+CHUNK = 2048
+UNITS_PER_CHUNK = CHUNK // UNIT
+CHUNKS_PER_BATCH = TIME // CHUNK
+CHUNKS = BATCH * CHUNKS_PER_BATCH
+UNITS = CHUNKS * UNITS_PER_CHUNK
+X_CHUNKS_IN_SBUF = 4
+UNITS_IN_PSUM = 2
+VECTOR_REGROUPS_ONE_IN = 8
+
+FLOPS = 2 * BATCH * TIME * CHANNELS * HEADS * P
+
+assert CHANNELS == P * PACK
+
+
+def quantise_weights(tc, nc, keep, Wq, Wk, Wv):
+    with ExitStack() as scope:
+        stage = scope.enter_context(tc.tile_pool(name="w_stage", bufs=1))
+        psum = scope.enter_context(tc.psum_pool(name="w_psum", bufs=2))
+
+        w_rows = stage.tile([P, HEADS, CHANNELS], BF16)
+        nc.scalar.dma_start(out=w_rows[:, 0, :], in_=Wq)
+        nc.scalar.dma_start(out=w_rows[:, 1, :], in_=Wk)
+        nc.scalar.dma_start(out=w_rows[:, 2:4, :], in_=Wv.rearrange("(h m) c -> m h c", h=2))
+
+        identity = stage.tile([P, P], F32)
+        make_identity(nc, identity[:])
+
+        w_words = w_rows[:].rearrange("m h c -> m (h c)").bitcast(F32).rearrange(
+            "m (h p e) -> m h e p", h=HEADS, e=2
+        )
+        w_grouped = stage.tile([P, HEADS * P * PACK], BF16, align_bytes=64)
+        w_grouped_words = w_grouped[:].bitcast(F32).rearrange("p (h m e) -> p h m e", h=HEADS, e=2)
+        for pair in range(HEADS // 2):
+            flipped = psum.tile([P, 2, 2, P], F32)
+            for i in range(2):
+                for e in range(2):
+                    nc.tensor.transpose(flipped[:, i, e, :], w_words[:, 2 * pair + i, e, :], identity[:])
+            nc.vector.tensor_copy(
+                out=w_grouped_words[:, 2 * pair : 2 * pair + 2, :, :],
+                in_=flipped[:].rearrange("p i e m -> p i m e"),
+            )
+
+        w_codes = keep.tile([P, HEADS * P], U32, align_bytes=64)
+        w_scales = keep.tile([P, HEADS * P], U8, align_bytes=64)
+        nc.vector.quantize_mx(out=w_codes[:].bitcast(FP8X4), scales=w_scales[:], in_=w_grouped[:])
+    return w_codes, w_scales
+
+
+def tile_selfattention_pa_t_kernel(tc, x, Wq, Wk, Wv, out_0, out_1, out_2):
+    nc = tc.nc
+    with ExitStack() as ctx:
+        ctx.enter_context(tc.manual_schedule())
+        keep = ctx.enter_context(tc.tile_pool(name="keep", bufs=1))
+        x_pool = ctx.enter_context(tc.tile_pool(name="x", bufs=X_CHUNKS_IN_SBUF))
+        work = ctx.enter_context(tc.tile_pool(name="work", bufs=3))
+        results = ctx.enter_context(tc.tile_pool(name="results", bufs=3))
+
+        x_tiles = {}
+        grouped_tiles = {}
+        sums_tiles = {}
+        result_tiles = {}
+
+        def load(n):
+            b, c = divmod(n, CHUNKS_PER_BATCH)
+            x_rows = x_pool.tile([P, PACK, CHUNK], BF16)
+            nc.sync.dma_start(
+                out=x_rows[:],
+                in_=x[b, :, c * CHUNK : (c + 1) * CHUNK].rearrange("(p j) t -> p j t", j=PACK),
+            )
+            x_tiles[n] = x_rows
+
+        def regroup(u):
+            n, i = divmod(u, UNITS_PER_CHUNK)
+            grouped = work.tile([P, UNIT, PACK], BF16, align_bytes=64)
+            regroup_out = grouped[:].rearrange("p (c i) j -> p c j i", i=4)
+            regroup_in = x_tiles[n][:, :, i * UNIT : (i + 1) * UNIT].rearrange("p j (c i) -> p c j i", i=4)
+            if u % VECTOR_REGROUPS_ONE_IN == 0:
+                nc.vector.tensor_copy(out=regroup_out, in_=regroup_in)
+            else:
+                nc.scalar.copy(out=regroup_out, in_=regroup_in)
+            grouped_tiles[u] = grouped
+
+        def multiply(u):
+            x_codes = work.tile([P, UNIT], U32, align_bytes=64)
+            x_scales = work.tile([P, UNIT], U8, align_bytes=64)
+            nc.vector.quantize_mx(
+                out=x_codes[:].bitcast(FP8X4),
+                scales=x_scales[:],
+                in_=grouped_tiles[u][:].rearrange("p t j -> p (t j)"),
+            )
+            for h in range(HEADS):
+                sums = psum.tile([P, UNIT], F32, tag="head%d" % h)
+                nc.tensor.matmul_mx(
+                    out=sums[:],
+                    lhsT=w_codes[:, h * P : (h + 1) * P].bitcast(FP8X4),
+                    lhsT_scale=w_scales[:, h * P : (h + 1) * P],
+                    rhs=x_codes[:].bitcast(FP8X4),
+                    rhs_scale=x_scales[:],
+                    start=True,
+                    stop=True,
+                )
+                sums_tiles[(u, h)] = sums
+
+        def drain(u):
+            n, i = divmod(u, UNITS_PER_CHUNK)
+            if i == 0:
+                q_out = results.tile([P, CHUNK], F32)
+                pooled = results.tile([P, POOLED_HEADS, CHUNK // WINDOW], F32)
+                result_tiles[n] = (q_out, pooled)
+            q_out, pooled = result_tiles[n]
+            nc.scalar.copy(out=q_out[:, i * UNIT : (i + 1) * UNIT], in_=sums_tiles[(u, 0)][:])
+            windows = slice(i * UNIT // WINDOW, (i + 1) * UNIT // WINDOW)
+            for h in range(1, HEADS):
+                nc.vector.tensor_reduce(
+                    out=pooled[:, h - 1, windows],
+                    in_=sums_tiles[(u, h)][:].rearrange("p (w i) -> p w i", i=WINDOW),
+                    axis=mybir.AxisListType.X,
+                    op=mybir.AluOpType.max,
+                )
+
+        def store(n):
+            b, c = divmod(n, CHUNKS_PER_BATCH)
+            q_out, pooled = result_tiles[n]
+            steps = slice(c * CHUNK, (c + 1) * CHUNK)
+            windows = slice(c * CHUNK // WINDOW, (c + 1) * CHUNK // WINDOW)
+            nc.sync.dma_start(out=out_0[b, :, steps], in_=q_out[:])
+            nc.sync.dma_start(out=out_1[b, :, windows], in_=pooled[:, 0, :])
+            nc.sync.dma_start(
+                out=out_2[b, :, windows].rearrange("(h m) w -> m h w", h=2), in_=pooled[:, 1:3, :]
+            )
+
+        for n in range(X_CHUNKS_IN_SBUF):
+            load(n)
+        w_codes, w_scales = quantise_weights(tc, nc, keep, Wq, Wk, Wv)
+        psum = ctx.enter_context(tc.psum_pool(name="sums", bufs=UNITS_IN_PSUM))
+
+        for s in range(UNITS + 2):
+            if s < UNITS:
+                regroup(s)
+                n, i = divmod(s, UNITS_PER_CHUNK)
+                if i == UNITS_PER_CHUNK - 1 and n + X_CHUNKS_IN_SBUF < CHUNKS:
+                    load(n + X_CHUNKS_IN_SBUF)
+            if 1 <= s <= UNITS:
+                multiply(s - 1)
+            if s >= 2:
+                drain(s - 2)
+                n, i = divmod(s - 2, UNITS_PER_CHUNK)
+                if i == UNITS_PER_CHUNK - 1:
+                    store(n)

@@ -23,7 +23,7 @@ CHUNKS = BATCH * CHUNKS_PER_BATCH
 UNITS = CHUNKS * UNITS_PER_CHUNK
 X_CHUNKS_IN_SBUF = 4
 UNITS_IN_PSUM = 2
-VECTOR_REGROUPS_ONE_IN = 8
+SCALAR_STEPS = 320
 
 FLOPS = 2 * BATCH * TIME * CHANNELS * HEADS * P
 
@@ -70,6 +70,7 @@ def tile_selfattention_pa_t_kernel(tc, x, Wq, Wk, Wv, out_0, out_1, out_2):
         ctx.enter_context(tc.manual_schedule())
         keep = ctx.enter_context(tc.tile_pool(name="keep", bufs=1))
         x_pool = ctx.enter_context(tc.tile_pool(name="x", bufs=X_CHUNKS_IN_SBUF))
+        grouped_pool = ctx.enter_context(tc.tile_pool(name="grouped", bufs=2))
         work = ctx.enter_context(tc.tile_pool(name="work", bufs=3))
         results = ctx.enter_context(tc.tile_pool(name="results", bufs=3))
 
@@ -78,24 +79,34 @@ def tile_selfattention_pa_t_kernel(tc, x, Wq, Wk, Wv, out_0, out_1, out_2):
         sums_tiles = {}
         result_tiles = {}
 
-        def load(n):
+        def load(n, pieces):
             b, c = divmod(n, CHUNKS_PER_BATCH)
             x_rows = x_pool.tile([P, PACK, CHUNK], BF16)
-            nc.sync.dma_start(
-                out=x_rows[:],
-                in_=x[b, :, c * CHUNK : (c + 1) * CHUNK].rearrange("(p j) t -> p j t", j=PACK),
-            )
+            length = CHUNK // pieces
+            for piece in range(pieces):
+                t0 = piece * length
+                nc.sync.dma_start(
+                    out=x_rows[:, :, t0 : t0 + length],
+                    in_=x[b, :, c * CHUNK + t0 : c * CHUNK + t0 + length].rearrange("(p j) t -> p j t", j=PACK),
+                )
             x_tiles[n] = x_rows
 
         def regroup(u):
             n, i = divmod(u, UNITS_PER_CHUNK)
-            grouped = work.tile([P, UNIT, PACK], BF16, align_bytes=64)
-            regroup_out = grouped[:].rearrange("p (c i) j -> p c j i", i=4)
-            regroup_in = x_tiles[n][:, :, i * UNIT : (i + 1) * UNIT].rearrange("p j (c i) -> p c j i", i=4)
-            if u % VECTOR_REGROUPS_ONE_IN == 0:
-                nc.vector.tensor_copy(out=regroup_out, in_=regroup_in)
-            else:
-                nc.scalar.copy(out=regroup_out, in_=regroup_in)
+            x_unit = x_tiles[n][:, :, i * UNIT : (i + 1) * UNIT]
+            grouped = grouped_pool.tile([P, UNIT, PACK], BF16, align_bytes=64)
+            nc.scalar.copy(
+                out=grouped[:, :SCALAR_STEPS, :].rearrange("p (c i) j -> p c j i", i=4),
+                in_=x_unit[:, :, :SCALAR_STEPS].rearrange("p j (c i) -> p c j i", i=4),
+            )
+            nc.gpsimd.tensor_scalar(
+                out=grouped[:, SCALAR_STEPS:, :],
+                in0=x_unit[:, :, SCALAR_STEPS:].rearrange("p j t -> p t j"),
+                scalar1=1.0,
+                scalar2=0.0,
+                op0=mybir.AluOpType.mult,
+                op1=mybir.AluOpType.add,
+            )
             grouped_tiles[u] = grouped
 
         def multiply(u):
@@ -136,20 +147,23 @@ def tile_selfattention_pa_t_kernel(tc, x, Wq, Wk, Wv, out_0, out_1, out_2):
                     op=mybir.AluOpType.max,
                 )
 
-        def store(n):
+        def store(n, first_unit, units):
             b, c = divmod(n, CHUNKS_PER_BATCH)
             q_out, pooled = result_tiles[n]
-            steps = slice(c * CHUNK, (c + 1) * CHUNK)
-            windows = slice(c * CHUNK // WINDOW, (c + 1) * CHUNK // WINDOW)
-            nc.sync.dma_start(out=out_0[b, :, steps], in_=q_out[:])
-            nc.sync.dma_start(out=out_1[b, :, windows], in_=pooled[:, 0, :])
+            t0, t1 = first_unit * UNIT, (first_unit + units) * UNIT
+            w0, w1 = t0 // WINDOW, t1 // WINDOW
+            steps = slice(c * CHUNK + t0, c * CHUNK + t1)
+            windows = slice(c * CHUNK // WINDOW + w0, c * CHUNK // WINDOW + w1)
+            nc.sync.dma_start(out=out_0[b, :, steps], in_=q_out[:, t0:t1])
+            nc.sync.dma_start(out=out_1[b, :, windows], in_=pooled[:, 0, w0:w1])
             nc.sync.dma_start(
-                out=out_2[b, :, windows].rearrange("(h m) w -> m h w", h=2), in_=pooled[:, 1:3, :]
+                out=out_2[b, :, windows].rearrange("(h m) w -> m h w", h=2), in_=pooled[:, 1:3, w0:w1]
             )
 
-        for n in range(X_CHUNKS_IN_SBUF):
-            load(n)
+        load(0, UNITS_PER_CHUNK)
         w_codes, w_scales = quantise_weights(tc, nc, keep, Wq, Wk, Wv)
+        for n in range(1, X_CHUNKS_IN_SBUF):
+            load(n, 1)
         psum = ctx.enter_context(tc.psum_pool(name="sums", bufs=UNITS_IN_PSUM))
 
         for s in range(UNITS + 2):
@@ -157,11 +171,13 @@ def tile_selfattention_pa_t_kernel(tc, x, Wq, Wk, Wv, out_0, out_1, out_2):
                 regroup(s)
                 n, i = divmod(s, UNITS_PER_CHUNK)
                 if i == UNITS_PER_CHUNK - 1 and n + X_CHUNKS_IN_SBUF < CHUNKS:
-                    load(n + X_CHUNKS_IN_SBUF)
+                    load(n + X_CHUNKS_IN_SBUF, 1)
             if 1 <= s <= UNITS:
                 multiply(s - 1)
             if s >= 2:
                 drain(s - 2)
                 n, i = divmod(s - 2, UNITS_PER_CHUNK)
-                if i == UNITS_PER_CHUNK - 1:
-                    store(n)
+                if n == CHUNKS - 1:
+                    store(n, i, 1)
+                elif i == UNITS_PER_CHUNK - 1:
+                    store(n, 0, UNITS_PER_CHUNK)

@@ -15,15 +15,15 @@ BATCH, CHANNELS, TIME = 4, 512, 4096
 WINDOW = 4
 HEADS = 4
 POOLED_HEADS = HEADS - 1
-UNIT = 512
+HALF = 512
+ROUND = 2 * HALF
 CHUNK = 2048
-UNITS_PER_CHUNK = CHUNK // UNIT
+ROUNDS_PER_CHUNK = CHUNK // ROUND
 CHUNKS_PER_BATCH = TIME // CHUNK
 CHUNKS = BATCH * CHUNKS_PER_BATCH
-UNITS = CHUNKS * UNITS_PER_CHUNK
+ROUNDS = CHUNKS * ROUNDS_PER_CHUNK
 X_CHUNKS_IN_SBUF = 4
-UNITS_IN_PSUM = 2
-SCALAR_STEPS = 320
+SCALAR_STEPS = 640
 
 FLOPS = 2 * BATCH * TIME * CHANNELS * HEADS * P
 
@@ -48,13 +48,13 @@ def quantise_weights(tc, nc, keep, Wq, Wk, Wv):
         )
         w_grouped = stage.tile([P, HEADS * P * PACK], BF16, align_bytes=64)
         w_grouped_words = w_grouped[:].bitcast(F32).rearrange("p (h m e) -> p h m e", h=HEADS, e=2)
-        for pair in range(HEADS // 2):
+        for bank in range(HEADS // 2):
             flipped = psum.tile([P, 2, 2, P], F32)
             for i in range(2):
                 for e in range(2):
-                    nc.tensor.transpose(flipped[:, i, e, :], w_words[:, 2 * pair + i, e, :], identity[:])
+                    nc.tensor.transpose(flipped[:, i, e, :], w_words[:, 2 * bank + i, e, :], identity[:])
             nc.vector.tensor_copy(
-                out=w_grouped_words[:, 2 * pair : 2 * pair + 2, :, :],
+                out=w_grouped_words[:, 2 * bank : 2 * bank + 2, :, :],
                 in_=flipped[:].rearrange("p i e m -> p i m e"),
             )
 
@@ -71,11 +71,12 @@ def tile_selfattention_pa_t_kernel(tc, x, Wq, Wk, Wv, out_0, out_1, out_2):
         keep = ctx.enter_context(tc.tile_pool(name="keep", bufs=1))
         x_pool = ctx.enter_context(tc.tile_pool(name="x", bufs=X_CHUNKS_IN_SBUF))
         grouped_pool = ctx.enter_context(tc.tile_pool(name="grouped", bufs=2))
-        work = ctx.enter_context(tc.tile_pool(name="work", bufs=3))
+        work = ctx.enter_context(tc.tile_pool(name="work", bufs=2))
         results = ctx.enter_context(tc.tile_pool(name="results", bufs=3))
 
         x_tiles = {}
         grouped_tiles = {}
+        quantised_tiles = {}
         sums_tiles = {}
         result_tiles = {}
 
@@ -91,93 +92,100 @@ def tile_selfattention_pa_t_kernel(tc, x, Wq, Wk, Wv, out_0, out_1, out_2):
                 )
             x_tiles[n] = x_rows
 
-        def regroup(u):
-            n, i = divmod(u, UNITS_PER_CHUNK)
-            x_unit = x_tiles[n][:, :, i * UNIT : (i + 1) * UNIT]
-            grouped = grouped_pool.tile([P, UNIT, PACK], BF16, align_bytes=64)
+        def regroup(r):
+            n, i = divmod(r, ROUNDS_PER_CHUNK)
+            x_round = x_tiles[n][:, :, i * ROUND : (i + 1) * ROUND]
+            grouped = grouped_pool.tile([P, ROUND, PACK], BF16, align_bytes=64)
             nc.scalar.copy(
                 out=grouped[:, :SCALAR_STEPS, :].rearrange("p (c i) j -> p c j i", i=4),
-                in_=x_unit[:, :, :SCALAR_STEPS].rearrange("p j (c i) -> p c j i", i=4),
+                in_=x_round[:, :, :SCALAR_STEPS].rearrange("p j (c i) -> p c j i", i=4),
             )
             nc.gpsimd.tensor_scalar(
                 out=grouped[:, SCALAR_STEPS:, :],
-                in0=x_unit[:, :, SCALAR_STEPS:].rearrange("p j t -> p t j"),
+                in0=x_round[:, :, SCALAR_STEPS:].rearrange("p j t -> p t j"),
                 scalar1=1.0,
                 scalar2=0.0,
                 op0=mybir.AluOpType.mult,
                 op1=mybir.AluOpType.add,
             )
-            grouped_tiles[u] = grouped
+            grouped_tiles[r] = grouped
 
-        def multiply(u):
-            x_codes = work.tile([P, UNIT], U32, align_bytes=64)
-            x_scales = work.tile([P, UNIT], U8, align_bytes=64)
+        def quantise(r):
+            x_codes = work.tile([P, ROUND], U32, align_bytes=64)
+            x_scales = work.tile([P, ROUND], U8, align_bytes=64)
             nc.vector.quantize_mx(
                 out=x_codes[:].bitcast(FP8X4),
                 scales=x_scales[:],
-                in_=grouped_tiles[u][:].rearrange("p t j -> p (t j)"),
+                in_=grouped_tiles[r][:].rearrange("p t j -> p (t j)"),
             )
+            quantised_tiles[r] = (x_codes, x_scales)
+
+        def multiply(r, half):
+            x_codes, x_scales = quantised_tiles[r]
+            steps = slice(half * HALF, (half + 1) * HALF)
             for h in range(HEADS):
-                sums = psum.tile([P, UNIT], F32, tag="head%d" % h)
+                sums = psum.tile([P, HALF], F32, tag="head%d" % h)
                 nc.tensor.matmul_mx(
                     out=sums[:],
                     lhsT=w_codes[:, h * P : (h + 1) * P].bitcast(FP8X4),
                     lhsT_scale=w_scales[:, h * P : (h + 1) * P],
-                    rhs=x_codes[:].bitcast(FP8X4),
-                    rhs_scale=x_scales[:],
+                    rhs=x_codes[:, steps].bitcast(FP8X4),
+                    rhs_scale=x_scales[:, steps],
                     start=True,
                     stop=True,
                 )
-                sums_tiles[(u, h)] = sums
+                sums_tiles[(r, half, h)] = sums
 
-        def drain(u):
-            n, i = divmod(u, UNITS_PER_CHUNK)
-            if i == 0:
+        def drain(r, half):
+            n, i = divmod(r, ROUNDS_PER_CHUNK)
+            if i == 0 and half == 0:
                 q_out = results.tile([P, CHUNK], F32)
                 pooled = results.tile([P, POOLED_HEADS, CHUNK // WINDOW], F32)
                 result_tiles[n] = (q_out, pooled)
             q_out, pooled = result_tiles[n]
-            nc.scalar.copy(out=q_out[:, i * UNIT : (i + 1) * UNIT], in_=sums_tiles[(u, 0)][:])
-            windows = slice(i * UNIT // WINDOW, (i + 1) * UNIT // WINDOW)
+            t0 = i * ROUND + half * HALF
+            nc.scalar.copy(out=q_out[:, t0 : t0 + HALF], in_=sums_tiles[(r, half, 0)][:])
             for h in range(1, HEADS):
                 nc.vector.tensor_reduce(
-                    out=pooled[:, h - 1, windows],
-                    in_=sums_tiles[(u, h)][:].rearrange("p (w i) -> p w i", i=WINDOW),
+                    out=pooled[:, h - 1, t0 // WINDOW : (t0 + HALF) // WINDOW],
+                    in_=sums_tiles[(r, half, h)][:].rearrange("p (w i) -> p w i", i=WINDOW),
                     axis=mybir.AxisListType.X,
                     op=mybir.AluOpType.max,
                 )
 
-        def store(n, first_unit, units):
+        def store(n, t0, length):
             b, c = divmod(n, CHUNKS_PER_BATCH)
             q_out, pooled = result_tiles[n]
-            t0, t1 = first_unit * UNIT, (first_unit + units) * UNIT
-            w0, w1 = t0 // WINDOW, t1 // WINDOW
-            steps = slice(c * CHUNK + t0, c * CHUNK + t1)
+            w0, w1 = t0 // WINDOW, (t0 + length) // WINDOW
+            steps = slice(c * CHUNK + t0, c * CHUNK + t0 + length)
             windows = slice(c * CHUNK // WINDOW + w0, c * CHUNK // WINDOW + w1)
-            nc.sync.dma_start(out=out_0[b, :, steps], in_=q_out[:, t0:t1])
+            nc.sync.dma_start(out=out_0[b, :, steps], in_=q_out[:, t0 : t0 + length])
             nc.sync.dma_start(out=out_1[b, :, windows], in_=pooled[:, 0, w0:w1])
             nc.sync.dma_start(
                 out=out_2[b, :, windows].rearrange("(h m) w -> m h w", h=2), in_=pooled[:, 1:3, w0:w1]
             )
 
-        load(0, UNITS_PER_CHUNK)
+        load(0, CHUNK // HALF)
         w_codes, w_scales = quantise_weights(tc, nc, keep, Wq, Wk, Wv)
         for n in range(1, X_CHUNKS_IN_SBUF):
             load(n, 1)
-        psum = ctx.enter_context(tc.psum_pool(name="sums", bufs=UNITS_IN_PSUM))
+        psum = ctx.enter_context(tc.psum_pool(name="sums", bufs=2))
 
-        for s in range(UNITS + 2):
-            if s < UNITS:
+        for s in range(ROUNDS + 2):
+            if s < ROUNDS:
                 regroup(s)
-                n, i = divmod(s, UNITS_PER_CHUNK)
-                if i == UNITS_PER_CHUNK - 1 and n + X_CHUNKS_IN_SBUF < CHUNKS:
+                n, i = divmod(s, ROUNDS_PER_CHUNK)
+                if i == ROUNDS_PER_CHUNK - 1 and n + X_CHUNKS_IN_SBUF < CHUNKS:
                     load(n + X_CHUNKS_IN_SBUF, 1)
-            if 1 <= s <= UNITS:
-                multiply(s - 1)
-            if s >= 2:
-                drain(s - 2)
-                n, i = divmod(s - 2, UNITS_PER_CHUNK)
-                if n == CHUNKS - 1:
-                    store(n, i, 1)
-                elif i == UNITS_PER_CHUNK - 1:
-                    store(n, 0, UNITS_PER_CHUNK)
+            if 1 <= s <= ROUNDS:
+                quantise(s - 1)
+            for half in range(2):
+                if s >= 2:
+                    drain(s - 2, half)
+                    n, i = divmod(s - 2, ROUNDS_PER_CHUNK)
+                    if n == CHUNKS - 1:
+                        store(n, i * ROUND + half * HALF, HALF)
+                    elif i == ROUNDS_PER_CHUNK - 1 and half == 1:
+                        store(n, 0, CHUNK)
+                if 1 <= s <= ROUNDS:
+                    multiply(s - 1, half)

@@ -14,16 +14,17 @@ PACK = 4
 BATCH, CHANNELS, TIME = 4, 512, 4096
 WINDOW = 4
 HEADS = 4
-POOLED_HEADS = HEADS - 1
-HALF = 512
-ROUND = 2 * HALF
+POOLED_HEADS = 3
+Q_HEAD = 3
+UNIT = 512
 CHUNK = 2048
-ROUNDS_PER_CHUNK = CHUNK // ROUND
+UNITS_PER_CHUNK = CHUNK // UNIT
 CHUNKS_PER_BATCH = TIME // CHUNK
 CHUNKS = BATCH * CHUNKS_PER_BATCH
-ROUNDS = CHUNKS * ROUNDS_PER_CHUNK
+UNITS = CHUNKS * UNITS_PER_CHUNK
 X_CHUNKS_IN_SBUF = 4
-SCALAR_STEPS = 640
+UNITS_IN_PSUM = 2
+SCALAR_STEPS = 320
 
 FLOPS = 2 * BATCH * TIME * CHANNELS * HEADS * P
 
@@ -36,9 +37,9 @@ def quantise_weights(tc, nc, keep, Wq, Wk, Wv):
         psum = scope.enter_context(tc.psum_pool(name="w_psum", bufs=2))
 
         w_rows = stage.tile([P, HEADS, CHANNELS], BF16)
-        nc.scalar.dma_start(out=w_rows[:, 0, :], in_=Wq)
-        nc.scalar.dma_start(out=w_rows[:, 1, :], in_=Wk)
-        nc.scalar.dma_start(out=w_rows[:, 2:4, :], in_=Wv.rearrange("(h m) c -> m h c", h=2))
+        nc.sync.dma_start(out=w_rows[:, 0, :], in_=Wk)
+        nc.sync.dma_start(out=w_rows[:, 1:3, :], in_=Wv.rearrange("(h m) c -> m h c", h=2))
+        nc.sync.dma_start(out=w_rows[:, Q_HEAD, :], in_=Wq)
 
         identity = stage.tile([P, P], F32)
         make_identity(nc, identity[:])
@@ -48,13 +49,13 @@ def quantise_weights(tc, nc, keep, Wq, Wk, Wv):
         )
         w_grouped = stage.tile([P, HEADS * P * PACK], BF16, align_bytes=64)
         w_grouped_words = w_grouped[:].bitcast(F32).rearrange("p (h m e) -> p h m e", h=HEADS, e=2)
-        for bank in range(HEADS // 2):
+        for pair in range(HEADS // 2):
             flipped = psum.tile([P, 2, 2, P], F32)
             for i in range(2):
                 for e in range(2):
-                    nc.tensor.transpose(flipped[:, i, e, :], w_words[:, 2 * bank + i, e, :], identity[:])
+                    nc.tensor.transpose(flipped[:, i, e, :], w_words[:, 2 * pair + i, e, :], identity[:])
             nc.vector.tensor_copy(
-                out=w_grouped_words[:, 2 * bank : 2 * bank + 2, :, :],
+                out=w_grouped_words[:, 2 * pair : 2 * pair + 2, :, :],
                 in_=flipped[:].rearrange("p i e m -> p i m e"),
             )
 
@@ -64,6 +65,15 @@ def quantise_weights(tc, nc, keep, Wq, Wk, Wv):
     return w_codes, w_scales
 
 
+def cut_into_pieces(fine_chunk):
+    pieces = []
+    for n in range(CHUNKS):
+        size = 1 if n == fine_chunk else UNITS_PER_CHUNK
+        for first in range(n * UNITS_PER_CHUNK, (n + 1) * UNITS_PER_CHUNK, size):
+            pieces.append((first, size))
+    return pieces
+
+
 def tile_selfattention_pa_t_kernel(tc, x, Wq, Wk, Wv, out_0, out_1, out_2):
     nc = tc.nc
     with ExitStack() as ctx:
@@ -71,121 +81,109 @@ def tile_selfattention_pa_t_kernel(tc, x, Wq, Wk, Wv, out_0, out_1, out_2):
         keep = ctx.enter_context(tc.tile_pool(name="keep", bufs=1))
         x_pool = ctx.enter_context(tc.tile_pool(name="x", bufs=X_CHUNKS_IN_SBUF))
         grouped_pool = ctx.enter_context(tc.tile_pool(name="grouped", bufs=2))
-        work = ctx.enter_context(tc.tile_pool(name="work", bufs=2))
+        work = ctx.enter_context(tc.tile_pool(name="work", bufs=3))
         results = ctx.enter_context(tc.tile_pool(name="results", bufs=3))
 
-        x_tiles = {}
+        loads = cut_into_pieces(0)
+        stores = cut_into_pieces(CHUNKS - 1)
+        store_of_unit = {first + i: (first, size) for first, size in stores for i in range(size)}
+
+        x_units = {}
         grouped_tiles = {}
-        quantised_tiles = {}
         sums_tiles = {}
         result_tiles = {}
 
-        def load(n, pieces):
-            b, c = divmod(n, CHUNKS_PER_BATCH)
-            x_rows = x_pool.tile([P, PACK, CHUNK], BF16)
-            length = CHUNK // pieces
-            for piece in range(pieces):
-                t0 = piece * length
-                nc.sync.dma_start(
-                    out=x_rows[:, :, t0 : t0 + length],
-                    in_=x[b, :, c * CHUNK + t0 : c * CHUNK + t0 + length].rearrange("(p j) t -> p j t", j=PACK),
-                )
-            x_tiles[n] = x_rows
+        def load(first, size):
+            b, t0 = divmod(first * UNIT, TIME)
+            x_rows = x_pool.tile([P, PACK, size * UNIT], BF16, tag="x%d" % size)
+            nc.sync.dma_start(
+                out=x_rows[:], in_=x[b, :, t0 : t0 + size * UNIT].rearrange("(p j) t -> p j t", j=PACK)
+            )
+            for i in range(size):
+                x_units[first + i] = x_rows[:, :, i * UNIT : (i + 1) * UNIT]
 
-        def regroup(r):
-            n, i = divmod(r, ROUNDS_PER_CHUNK)
-            x_round = x_tiles[n][:, :, i * ROUND : (i + 1) * ROUND]
-            grouped = grouped_pool.tile([P, ROUND, PACK], BF16, align_bytes=64)
+        def regroup(u):
+            grouped = grouped_pool.tile([P, UNIT, PACK], BF16, align_bytes=64)
             nc.scalar.copy(
                 out=grouped[:, :SCALAR_STEPS, :].rearrange("p (c i) j -> p c j i", i=4),
-                in_=x_round[:, :, :SCALAR_STEPS].rearrange("p j (c i) -> p c j i", i=4),
+                in_=x_units[u][:, :, :SCALAR_STEPS].rearrange("p j (c i) -> p c j i", i=4),
             )
             nc.gpsimd.tensor_scalar(
                 out=grouped[:, SCALAR_STEPS:, :],
-                in0=x_round[:, :, SCALAR_STEPS:].rearrange("p j t -> p t j"),
+                in0=x_units[u][:, :, SCALAR_STEPS:].rearrange("p j t -> p t j"),
                 scalar1=1.0,
                 scalar2=0.0,
                 op0=mybir.AluOpType.mult,
                 op1=mybir.AluOpType.add,
             )
-            grouped_tiles[r] = grouped
+            grouped_tiles[u] = grouped
 
-        def quantise(r):
-            x_codes = work.tile([P, ROUND], U32, align_bytes=64)
-            x_scales = work.tile([P, ROUND], U8, align_bytes=64)
+        def multiply(u):
+            x_codes = work.tile([P, UNIT], U32, align_bytes=64)
+            x_scales = work.tile([P, UNIT], U8, align_bytes=64)
             nc.vector.quantize_mx(
                 out=x_codes[:].bitcast(FP8X4),
                 scales=x_scales[:],
-                in_=grouped_tiles[r][:].rearrange("p t j -> p (t j)"),
+                in_=grouped_tiles[u][:].rearrange("p t j -> p (t j)"),
             )
-            quantised_tiles[r] = (x_codes, x_scales)
-
-        def multiply(r, half):
-            x_codes, x_scales = quantised_tiles[r]
-            steps = slice(half * HALF, (half + 1) * HALF)
             for h in range(HEADS):
-                sums = psum.tile([P, HALF], F32, tag="head%d" % h)
+                sums = psum.tile([P, UNIT], F32, tag="head%d" % h)
                 nc.tensor.matmul_mx(
                     out=sums[:],
                     lhsT=w_codes[:, h * P : (h + 1) * P].bitcast(FP8X4),
                     lhsT_scale=w_scales[:, h * P : (h + 1) * P],
-                    rhs=x_codes[:, steps].bitcast(FP8X4),
-                    rhs_scale=x_scales[:, steps],
+                    rhs=x_codes[:].bitcast(FP8X4),
+                    rhs_scale=x_scales[:],
                     start=True,
                     stop=True,
                 )
-                sums_tiles[(r, half, h)] = sums
+                sums_tiles[(u, h)] = sums
 
-        def drain(r, half):
-            n, i = divmod(r, ROUNDS_PER_CHUNK)
-            if i == 0 and half == 0:
-                q_out = results.tile([P, CHUNK], F32)
-                pooled = results.tile([P, POOLED_HEADS, CHUNK // WINDOW], F32)
-                result_tiles[n] = (q_out, pooled)
-            q_out, pooled = result_tiles[n]
-            t0 = i * ROUND + half * HALF
-            nc.scalar.copy(out=q_out[:, t0 : t0 + HALF], in_=sums_tiles[(r, half, 0)][:])
-            for h in range(1, HEADS):
+        def drain(u):
+            first, size = store_of_unit[u]
+            if u == first:
+                q_out = results.tile([P, size * UNIT], F32, tag="q%d" % size)
+                pooled = results.tile([P, POOLED_HEADS, size * UNIT // WINDOW], F32, tag="pooled%d" % size)
+                result_tiles[first] = (q_out, pooled)
+            q_out, pooled = result_tiles[first]
+            t0 = (u - first) * UNIT
+            nc.scalar.copy(out=q_out[:, t0 : t0 + UNIT], in_=sums_tiles[(u, Q_HEAD)][:])
+            for h in range(POOLED_HEADS):
                 nc.vector.tensor_reduce(
-                    out=pooled[:, h - 1, t0 // WINDOW : (t0 + HALF) // WINDOW],
-                    in_=sums_tiles[(r, half, h)][:].rearrange("p (w i) -> p w i", i=WINDOW),
+                    out=pooled[:, h, t0 // WINDOW : (t0 + UNIT) // WINDOW],
+                    in_=sums_tiles[(u, h)][:].rearrange("p (w i) -> p w i", i=WINDOW),
                     axis=mybir.AxisListType.X,
                     op=mybir.AluOpType.max,
                 )
 
-        def store(n, t0, length):
-            b, c = divmod(n, CHUNKS_PER_BATCH)
-            q_out, pooled = result_tiles[n]
-            w0, w1 = t0 // WINDOW, (t0 + length) // WINDOW
-            steps = slice(c * CHUNK + t0, c * CHUNK + t0 + length)
-            windows = slice(c * CHUNK // WINDOW + w0, c * CHUNK // WINDOW + w1)
-            nc.sync.dma_start(out=out_0[b, :, steps], in_=q_out[:, t0 : t0 + length])
-            nc.sync.dma_start(out=out_1[b, :, windows], in_=pooled[:, 0, w0:w1])
+        def store(first, size):
+            b, t0 = divmod(first * UNIT, TIME)
+            q_out, pooled = result_tiles[first]
+            windows = slice(t0 // WINDOW, (t0 + size * UNIT) // WINDOW)
+            nc.sync.dma_start(out=out_0[b, :, t0 : t0 + size * UNIT], in_=q_out[:])
+            nc.sync.dma_start(out=out_1[b, :, windows], in_=pooled[:, 0, :])
             nc.sync.dma_start(
-                out=out_2[b, :, windows].rearrange("(h m) w -> m h w", h=2), in_=pooled[:, 1:3, w0:w1]
+                out=out_2[b, :, windows].rearrange("(h m) w -> m h w", h=2), in_=pooled[:, 1:3, :]
             )
 
-        load(0, CHUNK // HALF)
         w_codes, w_scales = quantise_weights(tc, nc, keep, Wq, Wk, Wv)
-        for n in range(1, X_CHUNKS_IN_SBUF):
-            load(n, 1)
-        psum = ctx.enter_context(tc.psum_pool(name="sums", bufs=2))
+        loads_at_once = UNITS_PER_CHUNK + X_CHUNKS_IN_SBUF
+        for first, size in loads[:loads_at_once]:
+            load(first, size)
+        load_after_unit = {
+            first + size - 1: later for (first, size), later in zip(loads[UNITS_PER_CHUNK:], loads[loads_at_once:])
+        }
+        psum = ctx.enter_context(tc.psum_pool(name="sums", bufs=UNITS_IN_PSUM))
 
-        for s in range(ROUNDS + 2):
-            if s < ROUNDS:
+        for s in range(UNITS + 2):
+            if s < UNITS:
                 regroup(s)
-                n, i = divmod(s, ROUNDS_PER_CHUNK)
-                if i == ROUNDS_PER_CHUNK - 1 and n + X_CHUNKS_IN_SBUF < CHUNKS:
-                    load(n + X_CHUNKS_IN_SBUF, 1)
-            if 1 <= s <= ROUNDS:
-                quantise(s - 1)
-            for half in range(2):
-                if s >= 2:
-                    drain(s - 2, half)
-                    n, i = divmod(s - 2, ROUNDS_PER_CHUNK)
-                    if n == CHUNKS - 1:
-                        store(n, i * ROUND + half * HALF, HALF)
-                    elif i == ROUNDS_PER_CHUNK - 1 and half == 1:
-                        store(n, 0, CHUNK)
-                if 1 <= s <= ROUNDS:
-                    multiply(s - 1, half)
+                if s in load_after_unit:
+                    load(*load_after_unit[s])
+            if 1 <= s <= UNITS:
+                multiply(s - 1)
+            if s >= 2:
+                drain(s - 2)
+                first, size = store_of_unit[s - 2]
+                if s - 2 == first + size - 1:
+                    store(first, size)

@@ -25,6 +25,8 @@ UNITS = CHUNKS * UNITS_PER_CHUNK
 X_CHUNKS_IN_SBUF = 4
 UNITS_IN_PSUM = 2
 SCALAR_STEPS = 320
+CHAINED_HEADS = 1
+UNITS_WHILE_EMPTYING = 2
 
 FLOPS = 2 * BATCH * TIME * CHANNELS * HEADS * P
 
@@ -83,6 +85,7 @@ def tile_selfattention_pa_t_kernel(tc, x, Wq, Wk, Wv, out_0, out_1, out_2):
         grouped_pool = ctx.enter_context(tc.tile_pool(name="grouped", bufs=2))
         work = ctx.enter_context(tc.tile_pool(name="work", bufs=3))
         results = ctx.enter_context(tc.tile_pool(name="results", bufs=3))
+        chain_pool = ctx.enter_context(tc.tile_pool(name="chain", bufs=3))
 
         loads = cut_into_pieces(0)
         stores = cut_into_pieces(CHUNKS - 1)
@@ -147,14 +150,35 @@ def tile_selfattention_pa_t_kernel(tc, x, Wq, Wk, Wv, out_0, out_1, out_2):
                 result_tiles[first] = (q_out, pooled)
             q_out, pooled = result_tiles[first]
             t0 = (u - first) * UNIT
-            nc.scalar.copy(out=q_out[:, t0 : t0 + UNIT], in_=sums_tiles[(u, Q_HEAD)][:])
-            for h in range(POOLED_HEADS):
-                nc.vector.tensor_reduce(
-                    out=pooled[:, h, t0 // WINDOW : (t0 + UNIT) // WINDOW],
-                    in_=sums_tiles[(u, h)][:].rearrange("p (w i) -> p w i", i=WINDOW),
-                    axis=mybir.AxisListType.X,
-                    op=mybir.AluOpType.max,
+            chained = POOLED_HEADS if u >= UNITS - UNITS_WHILE_EMPTYING else CHAINED_HEADS
+            alone = POOLED_HEADS - chained
+            windows = slice(t0 // WINDOW, (t0 + UNIT) // WINDOW)
+            links = [pooled[:, alone:POOLED_HEADS, windows]]
+            for i in range(1, WINDOW):
+                link = chain_pool.tile([P, POOLED_HEADS, UNIT // WINDOW], F32, tag="link%d" % i)
+                links.append(link[:, 0:chained, :])
+            for n in range(chained):
+                nc.scalar.copy(
+                    out=links[WINDOW - 1][:, n, :],
+                    in_=sums_tiles[(u, alone + n)][:].rearrange("p (w i) -> p i w", i=WINDOW)[:, WINDOW - 1, :],
                 )
+            nc.scalar.copy(out=q_out[:, t0 : t0 + UNIT], in_=sums_tiles[(u, Q_HEAD)][:])
+            for i in range(WINDOW - 2, -1, -1):
+                for n in range(chained):
+                    nc.vector.tensor_tensor(
+                        out=links[i][:, n, :],
+                        in0=sums_tiles[(u, alone + n)][:].rearrange("p (w i) -> p i w", i=WINDOW)[:, i, :],
+                        in1=links[i + 1][:, n, :],
+                        op=mybir.AluOpType.max,
+                    )
+                h = WINDOW - 2 - i
+                if h < alone:
+                    nc.vector.tensor_reduce(
+                        out=pooled[:, h, windows],
+                        in_=sums_tiles[(u, h)][:].rearrange("p (w i) -> p w i", i=WINDOW),
+                        axis=mybir.AxisListType.X,
+                        op=mybir.AluOpType.max,
+                    )
 
         def store(first, size):
             b, t0 = divmod(first * UNIT, TIME)

@@ -24,13 +24,16 @@ CHUNKS = BATCH * CHUNKS_PER_BATCH
 UNITS = CHUNKS * UNITS_PER_CHUNK
 X_CHUNKS_IN_SBUF = 4
 UNITS_IN_PSUM = 2
-SCALAR_STEPS = 320
-CHAINED_HEADS = 1
+SCALAR_STEPS = 224
+GPSIMD_STEPS = 160
+TENSOR_STEPS = 128
+CHAINED_HEADS = 2
 UNITS_WHILE_EMPTYING = 2
 
 FLOPS = 2 * BATCH * TIME * CHANNELS * HEADS * P
 
 assert CHANNELS == P * PACK
+assert SCALAR_STEPS + GPSIMD_STEPS + TENSOR_STEPS == UNIT
 
 
 def quantise_weights(tc, nc, keep, Wq, Wk, Wv):
@@ -86,15 +89,19 @@ def tile_selfattention_pa_t_kernel(tc, x, Wq, Wk, Wv, out_0, out_1, out_2):
         work = ctx.enter_context(tc.tile_pool(name="work", bufs=3))
         results = ctx.enter_context(tc.tile_pool(name="results", bufs=3))
         chain_pool = ctx.enter_context(tc.tile_pool(name="chain", bufs=3))
+        turned_pool = ctx.enter_context(tc.psum_pool(name="turned", bufs=1))
 
         loads = cut_into_pieces(0)
         stores = cut_into_pieces(CHUNKS - 1)
         store_of_unit = {first + i: (first, size) for first, size in stores for i in range(size)}
 
         x_units = {}
+        turned_tiles = {}
         grouped_tiles = {}
+        quantised = {}
         sums_tiles = {}
         result_tiles = {}
+        chains = {}
 
         def load(first, size):
             b, t0 = divmod(first * UNIT, TIME)
@@ -105,6 +112,17 @@ def tile_selfattention_pa_t_kernel(tc, x, Wq, Wk, Wv, out_0, out_1, out_2):
             for i in range(size):
                 x_units[first + i] = x_rows[:, :, i * UNIT : (i + 1) * UNIT]
 
+        def turn(u):
+            turned = turned_pool.tile([P, TENSOR_STEPS * PACK], BF16)
+            nc.tensor.matmul(
+                out=turned[:],
+                lhsT=identity[:],
+                rhs=x_units[u][:, :, SCALAR_STEPS + GPSIMD_STEPS :].rearrange("p j t -> p t j"),
+                start=True,
+                stop=True,
+            )
+            turned_tiles[u] = turned
+
         def regroup(u):
             grouped = grouped_pool.tile([P, UNIT, PACK], BF16, align_bytes=64)
             nc.scalar.copy(
@@ -112,8 +130,8 @@ def tile_selfattention_pa_t_kernel(tc, x, Wq, Wk, Wv, out_0, out_1, out_2):
                 in_=x_units[u][:, :, :SCALAR_STEPS].rearrange("p j (c i) -> p c j i", i=4),
             )
             nc.gpsimd.tensor_scalar(
-                out=grouped[:, SCALAR_STEPS:, :],
-                in0=x_units[u][:, :, SCALAR_STEPS:].rearrange("p j t -> p t j"),
+                out=grouped[:, SCALAR_STEPS : SCALAR_STEPS + GPSIMD_STEPS, :],
+                in0=x_units[u][:, :, SCALAR_STEPS : SCALAR_STEPS + GPSIMD_STEPS].rearrange("p j t -> p t j"),
                 scalar1=1.0,
                 scalar2=0.0,
                 op0=mybir.AluOpType.mult,
@@ -121,7 +139,13 @@ def tile_selfattention_pa_t_kernel(tc, x, Wq, Wk, Wv, out_0, out_1, out_2):
             )
             grouped_tiles[u] = grouped
 
-        def multiply(u):
+        def collect(u):
+            nc.scalar.copy(
+                out=grouped_tiles[u][:, SCALAR_STEPS + GPSIMD_STEPS :, :].rearrange("p t j -> p (t j)"),
+                in_=turned_tiles[u][:],
+            )
+
+        def quantise(u):
             x_codes = work.tile([P, UNIT], U32, align_bytes=64)
             x_scales = work.tile([P, UNIT], U8, align_bytes=64)
             nc.vector.quantize_mx(
@@ -129,8 +153,12 @@ def tile_selfattention_pa_t_kernel(tc, x, Wq, Wk, Wv, out_0, out_1, out_2):
                 scales=x_scales[:],
                 in_=grouped_tiles[u][:].rearrange("p t j -> p (t j)"),
             )
+            quantised[u] = (x_codes, x_scales)
+
+        def multiply(u):
+            x_codes, x_scales = quantised[u]
             for h in range(HEADS):
-                sums = psum.tile([P, UNIT], F32, tag="head%d" % h)
+                sums = psum.tile([P, UNIT], F32, tag="head%d" % h, bufs=UNITS_IN_PSUM if h != Q_HEAD else 1)
                 nc.tensor.matmul_mx(
                     out=sums[:],
                     lhsT=w_codes[:, h * P : (h + 1) * P].bitcast(FP8X4),
@@ -141,6 +169,19 @@ def tile_selfattention_pa_t_kernel(tc, x, Wq, Wk, Wv, out_0, out_1, out_2):
                     stop=True,
                 )
                 sums_tiles[(u, h)] = sums
+
+        def step_of_windows(u, h, i):
+            return sums_tiles[(u, h)][:].rearrange("p (w i) -> p i w", i=WINDOW)[:, i, :]
+
+        def link_up(u, i):
+            alone, links = chains[u]
+            for n in range(POOLED_HEADS - alone):
+                nc.vector.tensor_tensor(
+                    out=links[i][:, n, :],
+                    in0=step_of_windows(u, alone + n, i),
+                    in1=links[i + 1][:, n, :],
+                    op=mybir.AluOpType.max,
+                )
 
         def drain(u):
             first, size = store_of_unit[u]
@@ -157,38 +198,36 @@ def tile_selfattention_pa_t_kernel(tc, x, Wq, Wk, Wv, out_0, out_1, out_2):
             for i in range(1, WINDOW):
                 link = chain_pool.tile([P, POOLED_HEADS, UNIT // WINDOW], F32, tag="link%d" % i)
                 links.append(link[:, 0:chained, :])
+            chains[u] = (alone, links)
             for n in range(chained):
-                nc.scalar.copy(
-                    out=links[WINDOW - 1][:, n, :],
-                    in_=sums_tiles[(u, alone + n)][:].rearrange("p (w i) -> p i w", i=WINDOW)[:, WINDOW - 1, :],
-                )
+                nc.scalar.copy(out=links[WINDOW - 1][:, n, :], in_=step_of_windows(u, alone + n, WINDOW - 1))
             nc.scalar.copy(out=q_out[:, t0 : t0 + UNIT], in_=sums_tiles[(u, Q_HEAD)][:])
-            for i in range(WINDOW - 2, -1, -1):
-                for n in range(chained):
-                    nc.vector.tensor_tensor(
-                        out=links[i][:, n, :],
-                        in0=sums_tiles[(u, alone + n)][:].rearrange("p (w i) -> p i w", i=WINDOW)[:, i, :],
-                        in1=links[i + 1][:, n, :],
-                        op=mybir.AluOpType.max,
-                    )
-                h = WINDOW - 2 - i
-                if h < alone:
-                    nc.vector.tensor_reduce(
-                        out=pooled[:, h, windows],
-                        in_=sums_tiles[(u, h)][:].rearrange("p (w i) -> p w i", i=WINDOW),
-                        axis=mybir.AxisListType.X,
-                        op=mybir.AluOpType.max,
-                    )
+            link_up(u, 2)
+            for h in range(alone):
+                nc.vector.tensor_reduce(
+                    out=pooled[:, h, windows],
+                    in_=sums_tiles[(u, h)][:].rearrange("p (w i) -> p w i", i=WINDOW),
+                    axis=mybir.AxisListType.X,
+                    op=mybir.AluOpType.max,
+                )
+            link_up(u, 1)
 
-        def store(first, size):
+        def store_q(first, size):
             b, t0 = divmod(first * UNIT, TIME)
-            q_out, pooled = result_tiles[first]
+            nc.sync.dma_start(out=out_0[b, :, t0 : t0 + size * UNIT], in_=result_tiles[first][0][:])
+
+        def store_pooled(first, size):
+            b, t0 = divmod(first * UNIT, TIME)
+            pooled = result_tiles[first][1]
             windows = slice(t0 // WINDOW, (t0 + size * UNIT) // WINDOW)
-            nc.sync.dma_start(out=out_0[b, :, t0 : t0 + size * UNIT], in_=q_out[:])
             nc.sync.dma_start(out=out_1[b, :, windows], in_=pooled[:, 0, :])
             nc.sync.dma_start(
                 out=out_2[b, :, windows].rearrange("(h m) w -> m h w", h=2), in_=pooled[:, 1:3, :]
             )
+
+        def ends_a_piece(u):
+            first, size = store_of_unit[u]
+            return u == first + size - 1
 
         w_codes, w_scales = quantise_weights(tc, nc, keep, Wq, Wk, Wv)
         loads_at_once = UNITS_PER_CHUNK + X_CHUNKS_IN_SBUF
@@ -198,16 +237,28 @@ def tile_selfattention_pa_t_kernel(tc, x, Wq, Wk, Wv, out_0, out_1, out_2):
             first + size - 1: later for (first, size), later in zip(loads[UNITS_PER_CHUNK:], loads[loads_at_once:])
         }
         psum = ctx.enter_context(tc.psum_pool(name="sums", bufs=UNITS_IN_PSUM))
+        identity = keep.tile([P, P], BF16)
+        make_identity(nc, identity[:])
 
-        for s in range(UNITS + 2):
+        turn(0)
+        for s in range(UNITS + 3):
             if s < UNITS:
                 regroup(s)
                 if s in load_after_unit:
                     load(*load_after_unit[s])
             if 1 <= s <= UNITS:
+                quantise(s - 1)
+            if s >= 3:
+                link_up(s - 3, 0)
+                if ends_a_piece(s - 3):
+                    store_pooled(*store_of_unit[s - 3])
+            if 1 <= s <= UNITS:
                 multiply(s - 1)
-            if s >= 2:
+            if 2 <= s < UNITS + 2:
                 drain(s - 2)
-                first, size = store_of_unit[s - 2]
-                if s - 2 == first + size - 1:
-                    store(first, size)
+                if ends_a_piece(s - 2):
+                    store_q(*store_of_unit[s - 2])
+            if s < UNITS:
+                collect(s)
+            if s + 1 < UNITS:
+                turn(s + 1)

@@ -24,10 +24,10 @@ CHUNKS = BATCH * CHUNKS_PER_BATCH
 UNITS = CHUNKS * UNITS_PER_CHUNK
 X_CHUNKS_IN_SBUF = 4
 UNITS_IN_PSUM = 2
-SCALAR_STEPS = 224
-GPSIMD_STEPS = 160
+SCALAR_STEPS = 192
+GPSIMD_STEPS = 192
 TENSOR_STEPS = 128
-CHAINED_HEADS = 2
+CHAINED_HEADS = 3
 UNITS_WHILE_EMPTYING = 2
 
 FLOPS = 2 * BATCH * TIME * CHANNELS * HEADS * P

@@ -17,23 +17,23 @@ HEADS = 4
 POOLED_HEADS = 3
 Q_HEAD = 3
 UNIT = 512
+UNIT_WINDOWS = UNIT // WINDOW
 CHUNK = 2048
 UNITS_PER_CHUNK = CHUNK // UNIT
 CHUNKS_PER_BATCH = TIME // CHUNK
 CHUNKS = BATCH * CHUNKS_PER_BATCH
 UNITS = CHUNKS * UNITS_PER_CHUNK
+GROUPS = [1, 1] + [2] * 15
 X_CHUNKS_IN_SBUF = 4
-UNITS_IN_PSUM = 2
-SCALAR_STEPS = 192
-GPSIMD_STEPS = 192
-TENSOR_STEPS = 128
-CHAINED_HEADS = 3
-UNITS_WHILE_EMPTYING = 2
+SCALAR_WINDOWS = 40
+GPSIMD_WINDOWS = 48
+TENSOR_WINDOWS = 40
 
 FLOPS = 2 * BATCH * TIME * CHANNELS * HEADS * P
 
 assert CHANNELS == P * PACK
-assert SCALAR_STEPS + GPSIMD_STEPS + TENSOR_STEPS == UNIT
+assert SCALAR_WINDOWS + GPSIMD_WINDOWS + TENSOR_WINDOWS == UNIT_WINDOWS
+assert sum(GROUPS) == UNITS
 
 
 def quantise_weights(tc, nc, keep, Wq, Wk, Wv):
@@ -70,10 +70,10 @@ def quantise_weights(tc, nc, keep, Wq, Wk, Wv):
     return w_codes, w_scales
 
 
-def cut_into_pieces(fine_chunk):
+def cut_into_pieces(fine_chunk, fine_size):
     pieces = []
     for n in range(CHUNKS):
-        size = 1 if n == fine_chunk else UNITS_PER_CHUNK
+        size = fine_size if n == fine_chunk else UNITS_PER_CHUNK
         for first in range(n * UNITS_PER_CHUNK, (n + 1) * UNITS_PER_CHUNK, size):
             pieces.append((first, size))
     return pieces
@@ -86,20 +86,24 @@ def tile_selfattention_pa_t_kernel(tc, x, Wq, Wk, Wv, out_0, out_1, out_2):
         keep = ctx.enter_context(tc.tile_pool(name="keep", bufs=1))
         x_pool = ctx.enter_context(tc.tile_pool(name="x", bufs=X_CHUNKS_IN_SBUF))
         grouped_pool = ctx.enter_context(tc.tile_pool(name="grouped", bufs=2))
-        work = ctx.enter_context(tc.tile_pool(name="work", bufs=3))
+        work = ctx.enter_context(tc.tile_pool(name="work", bufs=5))
         results = ctx.enter_context(tc.tile_pool(name="results", bufs=3))
-        chain_pool = ctx.enter_context(tc.tile_pool(name="chain", bufs=3))
+        chain_pool = ctx.enter_context(tc.tile_pool(name="chain", bufs=2))
         turned_pool = ctx.enter_context(tc.psum_pool(name="turned", bufs=1))
 
-        loads = cut_into_pieces(0)
-        stores = cut_into_pieces(CHUNKS - 1)
+        loads = cut_into_pieces(0, 1)
+        stores = cut_into_pieces(CHUNKS - 1, 2)
         store_of_unit = {first + i: (first, size) for first, size in stores for i in range(size)}
+
+        group_first = [sum(GROUPS[:g]) for g in range(len(GROUPS))]
+        group_of_unit = {group_first[g] + i: g for g in range(len(GROUPS)) for i in range(GROUPS[g])}
 
         x_units = {}
         turned_tiles = {}
         grouped_tiles = {}
-        quantised = {}
+        codes = {}
         sums_tiles = {}
+        q_tiles = {}
         result_tiles = {}
         chains = {}
 
@@ -113,104 +117,132 @@ def tile_selfattention_pa_t_kernel(tc, x, Wq, Wk, Wv, out_0, out_1, out_2):
                 x_units[first + i] = x_rows[:, :, i * UNIT : (i + 1) * UNIT]
 
         def turn(u):
-            turned = turned_pool.tile([P, TENSOR_STEPS * PACK], BF16)
-            nc.tensor.matmul(
-                out=turned[:],
-                lhsT=identity[:],
-                rhs=x_units[u][:, :, SCALAR_STEPS + GPSIMD_STEPS :].rearrange("p j t -> p t j"),
-                start=True,
-                stop=True,
-            )
+            turned = turned_pool.tile([P, WINDOW, TENSOR_WINDOWS, PACK], BF16)
+            steps = slice((SCALAR_WINDOWS + GPSIMD_WINDOWS) * WINDOW, UNIT)
+            for j in range(0, PACK, 2):
+                nc.tensor.matmul(
+                    out=turned[:, :, :, j : j + 2].rearrange("p i w j -> p j w i"),
+                    lhsT=identity[:],
+                    rhs=x_units[u][:, j : j + 2, steps].rearrange("p j (w i) -> p j w i", i=WINDOW),
+                    start=True,
+                    stop=True,
+                )
             turned_tiles[u] = turned
 
-        def regroup(u):
-            grouped = grouped_pool.tile([P, UNIT, PACK], BF16, align_bytes=64)
+        def share(u, first, count):
+            g = group_of_unit[u]
+            w0 = (u - group_first[g]) * UNIT_WINDOWS + first
+            return grouped_tiles[g][:, :, w0 : w0 + count, :], x_units[u][:, :, first * WINDOW : (first + count) * WINDOW]
+
+        def regroup(u, quantised):
+            g = group_of_unit[u]
+            if u == group_first[g]:
+                grouped_tiles[g] = grouped_pool.tile([P, WINDOW, GROUPS[g] * UNIT_WINDOWS, PACK], BF16, name="grouped", align_bytes=64)
+            out, rows = share(u, 0, SCALAR_WINDOWS)
             nc.scalar.copy(
-                out=grouped[:, :SCALAR_STEPS, :].rearrange("p (c i) j -> p c j i", i=4),
-                in_=x_units[u][:, :, :SCALAR_STEPS].rearrange("p j (c i) -> p c j i", i=4),
+                out=out.rearrange("p i w j -> p w j i"), in_=rows.rearrange("p j (w i) -> p w j i", i=WINDOW)
             )
+            if quantised is not None:
+                word = work.tile([P, 1], U32, tag="word")
+                nc.gpsimd.tensor_copy(out=word[:], in_=codes[quantised][0][:, 0:1])
+            out, rows = share(u, SCALAR_WINDOWS, GPSIMD_WINDOWS)
             nc.gpsimd.tensor_scalar(
-                out=grouped[:, SCALAR_STEPS : SCALAR_STEPS + GPSIMD_STEPS, :],
-                in0=x_units[u][:, :, SCALAR_STEPS : SCALAR_STEPS + GPSIMD_STEPS].rearrange("p j t -> p t j"),
+                out=out,
+                in0=rows.rearrange("p j (w i) -> p i w j", i=WINDOW),
                 scalar1=1.0,
                 scalar2=0.0,
                 op0=mybir.AluOpType.mult,
                 op1=mybir.AluOpType.add,
             )
-            grouped_tiles[u] = grouped
 
         def collect(u):
-            nc.scalar.copy(
-                out=grouped_tiles[u][:, SCALAR_STEPS + GPSIMD_STEPS :, :].rearrange("p t j -> p (t j)"),
-                in_=turned_tiles[u][:],
-            )
+            out, rows = share(u, SCALAR_WINDOWS + GPSIMD_WINDOWS, TENSOR_WINDOWS)
+            nc.scalar.copy(out=out, in_=turned_tiles[u][:])
 
-        def quantise(u):
+        def quantise(g, part):
             x_codes = work.tile([P, UNIT], U32, align_bytes=64)
             x_scales = work.tile([P, UNIT], U8, align_bytes=64)
+            columns = slice(part * UNIT * PACK, (part + 1) * UNIT * PACK)
             nc.vector.quantize_mx(
                 out=x_codes[:].bitcast(FP8X4),
                 scales=x_scales[:],
-                in_=grouped_tiles[u][:].rearrange("p t j -> p (t j)"),
+                in_=grouped_tiles[g][:].rearrange("p i w j -> p (i w j)")[:, columns],
             )
-            quantised[u] = (x_codes, x_scales)
+            codes[(g, part)] = (x_codes, x_scales)
 
-        def multiply(u):
-            x_codes, x_scales = quantised[u]
-            for h in range(HEADS):
-                sums = psum.tile([P, UNIT], F32, tag="head%d" % h, bufs=UNITS_IN_PSUM if h != Q_HEAD else 1)
-                nc.tensor.matmul_mx(
-                    out=sums[:],
-                    lhsT=w_codes[:, h * P : (h + 1) * P].bitcast(FP8X4),
-                    lhsT_scale=w_scales[:, h * P : (h + 1) * P],
-                    rhs=x_codes[:].bitcast(FP8X4),
-                    rhs_scale=x_scales[:],
-                    start=True,
-                    stop=True,
+        def product(out, h, x_codes, x_scales):
+            nc.tensor.matmul_mx(
+                out=out,
+                lhsT=w_codes[:, h * P : (h + 1) * P].bitcast(FP8X4),
+                lhsT_scale=w_scales[:, h * P : (h + 1) * P],
+                rhs=x_codes.bitcast(FP8X4),
+                rhs_scale=x_scales,
+                start=True,
+                stop=True,
+            )
+
+        def multiply(g, part):
+            x_codes, x_scales = codes[(g, part)]
+            for h in range(POOLED_HEADS):
+                sums = psum.tile([P, UNIT], F32, tag="head%d" % h)
+                product(sums[:], h, x_codes[:], x_scales[:])
+                sums_tiles[(g, part, h)] = sums
+
+        def multiply_q(u):
+            g = group_of_unit[u]
+            q_sums = psum.tile([P, WINDOW, UNIT_WINDOWS], F32, tag="q", bufs=1)
+            for i in range(WINDOW):
+                column = i * GROUPS[g] * UNIT_WINDOWS + (u - group_first[g]) * UNIT_WINDOWS
+                part, at = divmod(column, UNIT)
+                x_codes, x_scales = codes[(g, part)]
+                product(
+                    q_sums[:, i, :], Q_HEAD, x_codes[:, at : at + UNIT_WINDOWS], x_scales[:, at : at + UNIT_WINDOWS]
                 )
-                sums_tiles[(u, h)] = sums
+            q_tiles[u] = q_sums
 
-        def step_of_windows(u, h, i):
-            return sums_tiles[(u, h)][:].rearrange("p (w i) -> p i w", i=WINDOW)[:, i, :]
-
-        def link_up(u, i):
-            alone, links = chains[u]
-            for n in range(POOLED_HEADS - alone):
-                nc.vector.tensor_tensor(
-                    out=links[i][:, n, :],
-                    in0=step_of_windows(u, alone + n, i),
-                    in1=links[i + 1][:, n, :],
-                    op=mybir.AluOpType.max,
-                )
-
-        def drain(u):
+        def result(u):
             first, size = store_of_unit[u]
-            if u == first:
+            if first not in result_tiles:
                 q_out = results.tile([P, size * UNIT], F32, tag="q%d" % size)
-                pooled = results.tile([P, POOLED_HEADS, size * UNIT // WINDOW], F32, tag="pooled%d" % size)
+                pooled = results.tile([P, POOLED_HEADS, size * UNIT_WINDOWS], F32, tag="pooled%d" % size)
                 result_tiles[first] = (q_out, pooled)
-            q_out, pooled = result_tiles[first]
-            t0 = (u - first) * UNIT
-            chained = POOLED_HEADS if u >= UNITS - UNITS_WHILE_EMPTYING else CHAINED_HEADS
-            alone = POOLED_HEADS - chained
-            windows = slice(t0 // WINDOW, (t0 + UNIT) // WINDOW)
-            links = [pooled[:, alone:POOLED_HEADS, windows]]
-            for i in range(1, WINDOW):
-                link = chain_pool.tile([P, POOLED_HEADS, UNIT // WINDOW], F32, tag="link%d" % i)
-                links.append(link[:, 0:chained, :])
-            chains[u] = (alone, links)
-            for n in range(chained):
-                nc.scalar.copy(out=links[WINDOW - 1][:, n, :], in_=step_of_windows(u, alone + n, WINDOW - 1))
-            nc.scalar.copy(out=q_out[:, t0 : t0 + UNIT], in_=sums_tiles[(u, Q_HEAD)][:])
-            link_up(u, 2)
-            for h in range(alone):
-                nc.vector.tensor_reduce(
-                    out=pooled[:, h, windows],
-                    in_=sums_tiles[(u, h)][:].rearrange("p (w i) -> p w i", i=WINDOW),
-                    axis=mybir.AxisListType.X,
-                    op=mybir.AluOpType.max,
-                )
-            link_up(u, 1)
+            return result_tiles[first], u - first
+
+        def drain_q(u):
+            (q_out, pooled), at = result(u)
+            nc.scalar.copy(
+                out=q_out[:, at * UNIT : (at + 1) * UNIT].rearrange("p (w i) -> p w i", i=WINDOW),
+                in_=q_tiles[u][:].rearrange("p i w -> p w i"),
+            )
+            first, size = store_of_unit[u]
+            if u == first + size - 1:
+                store_q(first, size)
+
+        def place(g, h, i):
+            windows = GROUPS[g] * UNIT_WINDOWS
+            part, at = divmod(i * windows, UNIT)
+            return sums_tiles[(g, part, h)][:, at : at + windows]
+
+        def copy_last_place(g, h):
+            windows = GROUPS[g] * UNIT_WINDOWS
+            if h == 0:
+                (q_out, pooled), at = result(group_first[g])
+                links = [pooled[:, :, at * UNIT_WINDOWS : at * UNIT_WINDOWS + windows]]
+                for i in range(1, WINDOW):
+                    link = chain_pool.tile([P, POOLED_HEADS, windows], F32, tag="link%d" % i)
+                    links.append(link[:])
+                chains[g] = links
+            nc.scalar.copy(out=chains[g][WINDOW - 1][:, h, :], in_=place(g, h, WINDOW - 1))
+
+        def link_up(g, i, h):
+            links = chains[g]
+            nc.vector.tensor_tensor(
+                out=links[i][:, h, :], in0=place(g, h, i), in1=links[i + 1][:, h, :], op=mybir.AluOpType.max
+            )
+            last = group_first[g] + GROUPS[g] - 1
+            first, size = store_of_unit[last]
+            if i == 0 and h == POOLED_HEADS - 1 and last == first + size - 1:
+                store_pooled(first, size)
 
         def store_q(first, size):
             b, t0 = divmod(first * UNIT, TIME)
@@ -225,10 +257,6 @@ def tile_selfattention_pa_t_kernel(tc, x, Wq, Wk, Wv, out_0, out_1, out_2):
                 out=out_2[b, :, windows].rearrange("(h m) w -> m h w", h=2), in_=pooled[:, 1:3, :]
             )
 
-        def ends_a_piece(u):
-            first, size = store_of_unit[u]
-            return u == first + size - 1
-
         w_codes, w_scales = quantise_weights(tc, nc, keep, Wq, Wk, Wv)
         loads_at_once = UNITS_PER_CHUNK + X_CHUNKS_IN_SBUF
         for first, size in loads[:loads_at_once]:
@@ -236,29 +264,49 @@ def tile_selfattention_pa_t_kernel(tc, x, Wq, Wk, Wv, out_0, out_1, out_2):
         load_after_unit = {
             first + size - 1: later for (first, size), later in zip(loads[UNITS_PER_CHUNK:], loads[loads_at_once:])
         }
-        psum = ctx.enter_context(tc.psum_pool(name="sums", bufs=UNITS_IN_PSUM))
+        psum = ctx.enter_context(tc.psum_pool(name="sums", bufs=2))
         identity = keep.tile([P, P], BF16)
         make_identity(nc, identity[:])
 
+        quantise_at, copy_first_at, copy_last_at, links_at, q_at = {}, {}, {}, {}, {}
+        heads = list(range(POOLED_HEADS))
+        for g, size in enumerate(GROUPS):
+            s = group_first[g] + size
+            for k in range(size):
+                quantise_at[s + k] = (g, size - 1 - k)
+            chain = [(g, i, h) for i in range(WINDOW - 2, -1, -1) for h in heads]
+            if size == 1:
+                copy_first_at[s + 1] = [(g, h) for h in heads]
+                links_at.setdefault(s + 1, []).extend(chain)
+                q_at[s + 1] = group_first[g]
+            else:
+                copy_last_at[s] = [(g, 0)]
+                copy_first_at[s + 1] = [(g, 1), (g, 2)]
+                links_at.setdefault(s + 1, []).extend(chain[:4])
+                links_at.setdefault(s + 2, []).extend(chain[4:])
+                q_at[s + 2] = group_first[g]
+                q_at[s + 3] = group_first[g] + 1
+
         turn(0)
-        for s in range(UNITS + 3):
+        for s in range(UNITS + 4):
+            if s in quantise_at:
+                quantise(*quantise_at[s])
+            for g, h in copy_first_at.get(s, []):
+                copy_last_place(g, h)
             if s < UNITS:
-                regroup(s)
+                regroup(s, quantise_at.get(s))
                 if s in load_after_unit:
                     load(*load_after_unit[s])
-            if 1 <= s <= UNITS:
-                quantise(s - 1)
-            if s >= 3:
-                link_up(s - 3, 0)
-                if ends_a_piece(s - 3):
-                    store_pooled(*store_of_unit[s - 3])
-            if 1 <= s <= UNITS:
-                multiply(s - 1)
-            if 2 <= s < UNITS + 2:
-                drain(s - 2)
-                if ends_a_piece(s - 2):
-                    store_q(*store_of_unit[s - 2])
-            if s < UNITS:
                 collect(s)
+            if s in q_at:
+                multiply_q(q_at[s])
+            if s in quantise_at:
+                multiply(*quantise_at[s])
             if s + 1 < UNITS:
                 turn(s + 1)
+            if s in q_at:
+                drain_q(q_at[s])
+            for g, i, h in links_at.get(s, []):
+                link_up(g, i, h)
+            for g, h in copy_last_at.get(s, []):
+                copy_last_place(g, h)

@@ -14,6 +14,8 @@ PACK = 4
 BATCH, CHANNELS, TIME = 4, 512, 4096
 WINDOW = 4
 HEADS = 4
+HALVES = 2
+PAIR = WINDOW // HALVES
 POOLED_HEADS = 3
 Q_HEAD = 3
 UNIT = 512
@@ -85,7 +87,7 @@ def tile_selfattention_pa_t_kernel(tc, x, Wq, Wk, Wv, out_0, out_1, out_2):
         ctx.enter_context(tc.manual_schedule())
         keep = ctx.enter_context(tc.tile_pool(name="keep", bufs=1))
         x_pool = ctx.enter_context(tc.tile_pool(name="x", bufs=X_CHUNKS_IN_SBUF))
-        grouped_pool = ctx.enter_context(tc.tile_pool(name="grouped", bufs=2))
+        grouped_pool = ctx.enter_context(tc.tile_pool(name="grouped", bufs=3))
         work = ctx.enter_context(tc.tile_pool(name="work", bufs=5))
         results = ctx.enter_context(tc.tile_pool(name="results", bufs=3))
         chain_pool = ctx.enter_context(tc.tile_pool(name="chain", bufs=2))
@@ -117,13 +119,13 @@ def tile_selfattention_pa_t_kernel(tc, x, Wq, Wk, Wv, out_0, out_1, out_2):
                 x_units[first + i] = x_rows[:, :, i * UNIT : (i + 1) * UNIT]
 
         def turn(u):
-            turned = turned_pool.tile([P, WINDOW, TENSOR_WINDOWS, PACK], BF16)
+            turned = turned_pool.tile([P, TENSOR_WINDOWS * WINDOW, PACK], BF16)
             steps = slice((SCALAR_WINDOWS + GPSIMD_WINDOWS) * WINDOW, UNIT)
             for j in range(0, PACK, 2):
                 nc.tensor.matmul(
-                    out=turned[:, :, :, j : j + 2].rearrange("p i w j -> p j w i"),
+                    out=turned[:, :, j : j + 2].rearrange("p t j -> p j t"),
                     lhsT=identity[:],
-                    rhs=x_units[u][:, j : j + 2, steps].rearrange("p j (w i) -> p j w i", i=WINDOW),
+                    rhs=x_units[u][:, j : j + 2, steps],
                     start=True,
                     stop=True,
                 )
@@ -132,23 +134,26 @@ def tile_selfattention_pa_t_kernel(tc, x, Wq, Wk, Wv, out_0, out_1, out_2):
         def share(u, first, count):
             g = group_of_unit[u]
             w0 = (u - group_first[g]) * UNIT_WINDOWS + first
-            return grouped_tiles[g][:, :, w0 : w0 + count, :], x_units[u][:, :, first * WINDOW : (first + count) * WINDOW]
+            return grouped_tiles[g][:, :, w0 : w0 + count, :, :], x_units[u][:, :, first * WINDOW : (first + count) * WINDOW]
 
         def regroup(u, quantised):
             g = group_of_unit[u]
             if u == group_first[g]:
-                grouped_tiles[g] = grouped_pool.tile([P, WINDOW, GROUPS[g] * UNIT_WINDOWS, PACK], BF16, name="grouped", align_bytes=64)
+                grouped_tiles[g] = grouped_pool.tile(
+                    [P, HALVES, GROUPS[g] * UNIT_WINDOWS, PAIR, PACK], BF16, name="grouped", align_bytes=64
+                )
             out, rows = share(u, 0, SCALAR_WINDOWS)
             nc.scalar.copy(
-                out=out.rearrange("p i w j -> p w j i"), in_=rows.rearrange("p j (w i) -> p w j i", i=WINDOW)
+                out=out.rearrange("p s w i j -> p w j s i"),
+                in_=rows.rearrange("p j (w s i) -> p w j s i", s=HALVES, i=PAIR),
             )
             if quantised is not None:
                 word = work.tile([P, 1], U32, tag="word")
                 nc.gpsimd.tensor_copy(out=word[:], in_=codes[quantised][0][:, 0:1])
             out, rows = share(u, SCALAR_WINDOWS, GPSIMD_WINDOWS)
             nc.gpsimd.tensor_scalar(
-                out=out,
-                in0=rows.rearrange("p j (w i) -> p i w j", i=WINDOW),
+                out=out.rearrange("p s w i j -> p w s i j"),
+                in0=rows.rearrange("p j (w s i) -> p w s i j", s=HALVES, i=PAIR),
                 scalar1=1.0,
                 scalar2=0.0,
                 op0=mybir.AluOpType.mult,
@@ -157,7 +162,10 @@ def tile_selfattention_pa_t_kernel(tc, x, Wq, Wk, Wv, out_0, out_1, out_2):
 
         def collect(u):
             out, rows = share(u, SCALAR_WINDOWS + GPSIMD_WINDOWS, TENSOR_WINDOWS)
-            nc.scalar.copy(out=out, in_=turned_tiles[u][:])
+            nc.scalar.copy(
+                out=out.rearrange("p s w i j -> p s w (i j)"),
+                in_=turned_tiles[u][:].rearrange("p (w s i) j -> p s w (i j)", s=HALVES, i=PAIR),
+            )
 
         def quantise(g, part):
             x_codes = work.tile([P, UNIT], U32, align_bytes=64)
@@ -166,7 +174,7 @@ def tile_selfattention_pa_t_kernel(tc, x, Wq, Wk, Wv, out_0, out_1, out_2):
             nc.vector.quantize_mx(
                 out=x_codes[:].bitcast(FP8X4),
                 scales=x_scales[:],
-                in_=grouped_tiles[g][:].rearrange("p i w j -> p (i w j)")[:, columns],
+                in_=grouped_tiles[g][:].rearrange("p s w i j -> p (s w i j)")[:, columns],
             )
             codes[(g, part)] = (x_codes, x_scales)
 
@@ -190,13 +198,17 @@ def tile_selfattention_pa_t_kernel(tc, x, Wq, Wk, Wv, out_0, out_1, out_2):
 
         def multiply_q(u):
             g = group_of_unit[u]
-            q_sums = psum.tile([P, WINDOW, UNIT_WINDOWS], F32, tag="q", bufs=1)
-            for i in range(WINDOW):
-                column = i * GROUPS[g] * UNIT_WINDOWS + (u - group_first[g]) * UNIT_WINDOWS
+            q_sums = psum.tile([P, HALVES, UNIT_WINDOWS, PAIR], F32, tag="q", bufs=1)
+            run = UNIT_WINDOWS * PAIR
+            for half in range(HALVES):
+                column = (half * GROUPS[g] + u - group_first[g]) * run
                 part, at = divmod(column, UNIT)
                 x_codes, x_scales = codes[(g, part)]
                 product(
-                    q_sums[:, i, :], Q_HEAD, x_codes[:, at : at + UNIT_WINDOWS], x_scales[:, at : at + UNIT_WINDOWS]
+                    q_sums[:, half, :, :].rearrange("p w i -> p (w i)"),
+                    Q_HEAD,
+                    x_codes[:, at : at + run],
+                    x_scales[:, at : at + run],
                 )
             q_tiles[u] = q_sums
 
@@ -211,8 +223,8 @@ def tile_selfattention_pa_t_kernel(tc, x, Wq, Wk, Wv, out_0, out_1, out_2):
         def drain_q(u):
             (q_out, pooled), at = result(u)
             nc.scalar.copy(
-                out=q_out[:, at * UNIT : (at + 1) * UNIT].rearrange("p (w i) -> p w i", i=WINDOW),
-                in_=q_tiles[u][:].rearrange("p i w -> p w i"),
+                out=q_out[:, at * UNIT : (at + 1) * UNIT].rearrange("p (w s i) -> p w s i", s=HALVES, i=PAIR),
+                in_=q_tiles[u][:].rearrange("p s w i -> p w s i"),
             )
             first, size = store_of_unit[u]
             if u == first + size - 1:
@@ -220,8 +232,10 @@ def tile_selfattention_pa_t_kernel(tc, x, Wq, Wk, Wv, out_0, out_1, out_2):
 
         def place(g, h, i):
             windows = GROUPS[g] * UNIT_WINDOWS
-            part, at = divmod(i * windows, UNIT)
-            return sums_tiles[(g, part, h)][:, at : at + windows]
+            half, which = divmod(i, PAIR)
+            part, at = divmod(half * windows * PAIR, UNIT)
+            pairs = sums_tiles[(g, part, h)][:, at : at + windows * PAIR].rearrange("p (w i) -> p i w", i=PAIR)
+            return pairs[:, which, :]
 
         def copy_last_place(g, h):
             windows = GROUPS[g] * UNIT_WINDOWS
@@ -268,10 +282,15 @@ def tile_selfattention_pa_t_kernel(tc, x, Wq, Wk, Wv, out_0, out_1, out_2):
         identity = keep.tile([P, P], BF16)
         make_identity(nc, identity[:])
 
-        quantise_at, copy_first_at, copy_last_at, links_at, q_at = {}, {}, {}, {}, {}
+        regroup_at, quantise_at, copy_first_at, copy_last_at, links_at, q_at = {}, {}, {}, {}, {}, {}
         heads = list(range(POOLED_HEADS))
+        step = 0
+        for u in range(UNITS):
+            regroup_at.setdefault(step, []).append(u)
+            if u not in (1, 3):
+                step += 1
+        s = 1
         for g, size in enumerate(GROUPS):
-            s = group_first[g] + size
             for k in range(size):
                 quantise_at[s + k] = (g, size - 1 - k)
             chain = [(g, i, h) for i in range(WINDOW - 2, -1, -1) for h in heads]
@@ -286,6 +305,7 @@ def tile_selfattention_pa_t_kernel(tc, x, Wq, Wk, Wv, out_0, out_1, out_2):
                 links_at.setdefault(s + 2, []).extend(chain[4:])
                 q_at[s + 2] = group_first[g]
                 q_at[s + 3] = group_first[g] + 1
+            s += size
 
         turn(0)
         for s in range(UNITS + 4):
@@ -293,17 +313,20 @@ def tile_selfattention_pa_t_kernel(tc, x, Wq, Wk, Wv, out_0, out_1, out_2):
                 quantise(*quantise_at[s])
             for g, h in copy_first_at.get(s, []):
                 copy_last_place(g, h)
-            if s < UNITS:
-                regroup(s, quantise_at.get(s))
-                if s in load_after_unit:
-                    load(*load_after_unit[s])
-                collect(s)
+            for u in regroup_at.get(s, []):
+                regroup(u, quantise_at.get(s) if u == regroup_at[s][0] else None)
+                if u in load_after_unit:
+                    load(*load_after_unit[u])
+                collect(u)
+                if u == regroup_at[s][-1]:
+                    break
+                turn(u + 1)
             if s in q_at:
                 multiply_q(q_at[s])
             if s in quantise_at:
                 multiply(*quantise_at[s])
-            if s + 1 < UNITS:
-                turn(s + 1)
+            if s + 1 in regroup_at:
+                turn(regroup_at[s + 1][0])
             if s in q_at:
                 drain_q(q_at[s])
             for g, i, h in links_at.get(s, []):

@@ -27,8 +27,8 @@ CHUNKS = BATCH * CHUNKS_PER_BATCH
 UNITS = CHUNKS * UNITS_PER_CHUNK
 GROUPS = [1, 1] + [2] * 15
 X_CHUNKS_IN_SBUF = 4
-SCALAR_WINDOWS = 40
-GPSIMD_WINDOWS = 48
+SCALAR_WINDOWS = 36
+GPSIMD_WINDOWS = 52
 TENSOR_WINDOWS = 40
 
 FLOPS = 2 * BATCH * TIME * CHANNELS * HEADS * P
@@ -72,12 +72,12 @@ def quantise_weights(tc, nc, keep, Wq, Wk, Wv):
     return w_codes, w_scales
 
 
-def cut_into_pieces(fine_chunk, fine_size):
-    pieces = []
-    for n in range(CHUNKS):
-        size = fine_size if n == fine_chunk else UNITS_PER_CHUNK
-        for first in range(n * UNITS_PER_CHUNK, (n + 1) * UNITS_PER_CHUNK, size):
-            pieces.append((first, size))
+def cut_into_pieces(sizes):
+    pieces, first = [], 0
+    while first < UNITS:
+        size = sizes.get(first, UNITS_PER_CHUNK)
+        pieces.append((first, size))
+        first += size
     return pieces
 
 
@@ -93,8 +93,8 @@ def tile_selfattention_pa_t_kernel(tc, x, Wq, Wk, Wv, out_0, out_1, out_2):
         chain_pool = ctx.enter_context(tc.tile_pool(name="chain", bufs=2))
         turned_pool = ctx.enter_context(tc.psum_pool(name="turned", bufs=1))
 
-        loads = cut_into_pieces(0, 1)
-        stores = cut_into_pieces(CHUNKS - 1, 2)
+        loads = cut_into_pieces({0: 1, 1: 1, 2: 1, 3: 1, 4: 2, 6: 2})
+        stores = cut_into_pieces({UNITS - 4: 2, UNITS - 2: 2})
         store_of_unit = {first + i: (first, size) for first, size in stores for i in range(size)}
 
         group_first = [sum(GROUPS[:g]) for g in range(len(GROUPS))]
@@ -111,7 +111,7 @@ def tile_selfattention_pa_t_kernel(tc, x, Wq, Wk, Wv, out_0, out_1, out_2):
 
         def load(first, size):
             b, t0 = divmod(first * UNIT, TIME)
-            x_rows = x_pool.tile([P, PACK, size * UNIT], BF16, tag="x%d" % size)
+            x_rows = x_pool.tile([P, PACK, size * UNIT], BF16, tag="x%d" % size, bufs=2 if size == 2 else X_CHUNKS_IN_SBUF)
             nc.sync.dma_start(
                 out=x_rows[:], in_=x[b, :, t0 : t0 + size * UNIT].rearrange("(p j) t -> p j t", j=PACK)
             )
@@ -136,7 +136,7 @@ def tile_selfattention_pa_t_kernel(tc, x, Wq, Wk, Wv, out_0, out_1, out_2):
             w0 = (u - group_first[g]) * UNIT_WINDOWS + first
             return grouped_tiles[g][:, :, w0 : w0 + count, :, :], x_units[u][:, :, first * WINDOW : (first + count) * WINDOW]
 
-        def regroup(u, quantised):
+        def regroup(u):
             g = group_of_unit[u]
             if u == group_first[g]:
                 grouped_tiles[g] = grouped_pool.tile(
@@ -147,9 +147,6 @@ def tile_selfattention_pa_t_kernel(tc, x, Wq, Wk, Wv, out_0, out_1, out_2):
                 out=out.rearrange("p s w i j -> p w j s i"),
                 in_=rows.rearrange("p j (w s i) -> p w j s i", s=HALVES, i=PAIR),
             )
-            if quantised is not None:
-                word = work.tile([P, 1], U32, tag="word")
-                nc.gpsimd.tensor_copy(out=word[:], in_=codes[quantised][0][:, 0:1])
             out, rows = share(u, SCALAR_WINDOWS, GPSIMD_WINDOWS)
             nc.gpsimd.tensor_scalar(
                 out=out.rearrange("p s w i j -> p w s i j"),
@@ -272,12 +269,13 @@ def tile_selfattention_pa_t_kernel(tc, x, Wq, Wk, Wv, out_0, out_1, out_2):
             )
 
         w_codes, w_scales = quantise_weights(tc, nc, keep, Wq, Wk, Wv)
-        loads_at_once = UNITS_PER_CHUNK + X_CHUNKS_IN_SBUF
-        for first, size in loads[:loads_at_once]:
-            load(first, size)
-        load_after_unit = {
-            first + size - 1: later for (first, size), later in zip(loads[UNITS_PER_CHUNK:], loads[loads_at_once:])
-        }
+        load_after_unit = {}
+        for first, size in loads:
+            after = first - X_CHUNKS_IN_SBUF * UNITS_PER_CHUNK + UNITS_PER_CHUNK - 1
+            if after < 0:
+                load(first, size)
+            else:
+                load_after_unit[after] = (first, size)
         psum = ctx.enter_context(tc.psum_pool(name="sums", bufs=2))
         identity = keep.tile([P, P], BF16)
         make_identity(nc, identity[:])
@@ -314,7 +312,7 @@ def tile_selfattention_pa_t_kernel(tc, x, Wq, Wk, Wv, out_0, out_1, out_2):
             for g, h in copy_first_at.get(s, []):
                 copy_last_place(g, h)
             for u in regroup_at.get(s, []):
-                regroup(u, quantise_at.get(s) if u == regroup_at[s][0] else None)
+                regroup(u)
                 if u in load_after_unit:
                     load(*load_after_unit[u])
                 collect(u)

@@ -27,14 +27,14 @@ CHUNKS = BATCH * CHUNKS_PER_BATCH
 UNITS = CHUNKS * UNITS_PER_CHUNK
 GROUPS = [1, 1] + [2] * 15
 X_CHUNKS_IN_SBUF = 4
-SCALAR_WINDOWS = 36
-GPSIMD_WINDOWS = 52
-TENSOR_WINDOWS = 40
+SHARES = (36, 0, 56, 36)
+FIRST_SHARES = (40, 64, 0, 24)
+FIRST_UNITS = 2
 
 FLOPS = 2 * BATCH * TIME * CHANNELS * HEADS * P
 
 assert CHANNELS == P * PACK
-assert SCALAR_WINDOWS + GPSIMD_WINDOWS + TENSOR_WINDOWS == UNIT_WINDOWS
+assert sum(SHARES) == sum(FIRST_SHARES) == UNIT_WINDOWS
 assert sum(GROUPS) == UNITS
 
 
@@ -61,7 +61,8 @@ def quantise_weights(tc, nc, keep, Wq, Wk, Wv):
             for i in range(2):
                 for e in range(2):
                     nc.tensor.transpose(flipped[:, i, e, :], w_words[:, 2 * pair + i, e, :], identity[:])
-            nc.vector.tensor_copy(
+            copy = nc.scalar.copy if pair == 0 else nc.vector.tensor_copy
+            copy(
                 out=w_grouped_words[:, 2 * pair : 2 * pair + 2, :, :],
                 in_=flipped[:].rearrange("p i e m -> p i m e"),
             )
@@ -94,8 +95,10 @@ def tile_selfattention_pa_t_kernel(tc, x, Wq, Wk, Wv, out_0, out_1, out_2):
         turned_pool = ctx.enter_context(tc.psum_pool(name="turned", bufs=1))
 
         loads = cut_into_pieces({0: 1, 1: 1, 2: 1, 3: 1, 4: 2, 6: 2})
-        stores = cut_into_pieces({UNITS - 4: 2, UNITS - 2: 2})
-        store_of_unit = {first + i: (first, size) for first, size in stores for i in range(size)}
+        q_pieces = cut_into_pieces({UNITS - 4: 2, UNITS - 2: 1, UNITS - 1: 1})
+        pooled_pieces = cut_into_pieces({UNITS - 4: 2, UNITS - 2: 2})
+        q_piece_of_unit = {first + i: (first, size) for first, size in q_pieces for i in range(size)}
+        pooled_piece_of_unit = {first + i: (first, size) for first, size in pooled_pieces for i in range(size)}
 
         group_first = [sum(GROUPS[:g]) for g in range(len(GROUPS))]
         group_of_unit = {group_first[g] + i: g for g in range(len(GROUPS)) for i in range(GROUPS[g])}
@@ -106,7 +109,7 @@ def tile_selfattention_pa_t_kernel(tc, x, Wq, Wk, Wv, out_0, out_1, out_2):
         codes = {}
         sums_tiles = {}
         q_tiles = {}
-        result_tiles = {}
+        q_out_tiles, pooled_tiles = {}, {}
         chains = {}
 
         def load(first, size):
@@ -118,23 +121,26 @@ def tile_selfattention_pa_t_kernel(tc, x, Wq, Wk, Wv, out_0, out_1, out_2):
             for i in range(size):
                 x_units[first + i] = x_rows[:, :, i * UNIT : (i + 1) * UNIT]
 
+        def share(u, engine):
+            shares = FIRST_SHARES if u < FIRST_UNITS else SHARES
+            first, count = sum(shares[:engine]), shares[engine]
+            g = group_of_unit[u]
+            w0 = (u - group_first[g]) * UNIT_WINDOWS + first
+            out = grouped_tiles[g][:, :, w0 : w0 + count, :, :] if g in grouped_tiles else None
+            return out, x_units[u][:, :, first * WINDOW : (first + count) * WINDOW], count
+
         def turn(u):
-            turned = turned_pool.tile([P, TENSOR_WINDOWS * WINDOW, PACK], BF16)
-            steps = slice((SCALAR_WINDOWS + GPSIMD_WINDOWS) * WINDOW, UNIT)
+            out, rows, count = share(u, 3)
+            turned = turned_pool.tile([P, count * WINDOW, PACK], BF16)
             for j in range(0, PACK, 2):
                 nc.tensor.matmul(
                     out=turned[:, :, j : j + 2].rearrange("p t j -> p j t"),
                     lhsT=identity[:],
-                    rhs=x_units[u][:, j : j + 2, steps],
+                    rhs=rows[:, j : j + 2, :],
                     start=True,
                     stop=True,
                 )
             turned_tiles[u] = turned
-
-        def share(u, first, count):
-            g = group_of_unit[u]
-            w0 = (u - group_first[g]) * UNIT_WINDOWS + first
-            return grouped_tiles[g][:, :, w0 : w0 + count, :, :], x_units[u][:, :, first * WINDOW : (first + count) * WINDOW]
 
         def regroup(u):
             g = group_of_unit[u]
@@ -142,23 +148,30 @@ def tile_selfattention_pa_t_kernel(tc, x, Wq, Wk, Wv, out_0, out_1, out_2):
                 grouped_tiles[g] = grouped_pool.tile(
                     [P, HALVES, GROUPS[g] * UNIT_WINDOWS, PAIR, PACK], BF16, name="grouped", align_bytes=64
                 )
-            out, rows = share(u, 0, SCALAR_WINDOWS)
+            out, rows, count = share(u, 0)
             nc.scalar.copy(
-                out=out.rearrange("p s w i j -> p w j s i"),
-                in_=rows.rearrange("p j (w s i) -> p w j s i", s=HALVES, i=PAIR),
+                out=out.rearrange("p s w i j -> p w s j i"),
+                in_=rows.rearrange("p j (w s i) -> p w s j i", s=HALVES, i=PAIR),
             )
-            out, rows = share(u, SCALAR_WINDOWS, GPSIMD_WINDOWS)
-            nc.gpsimd.tensor_scalar(
-                out=out.rearrange("p s w i j -> p w s i j"),
-                in0=rows.rearrange("p j (w s i) -> p w s i j", s=HALVES, i=PAIR),
-                scalar1=1.0,
-                scalar2=0.0,
-                op0=mybir.AluOpType.mult,
-                op1=mybir.AluOpType.add,
-            )
+            out, rows, count = share(u, 1)
+            if count:
+                nc.vector.tensor_copy(
+                    out=out.rearrange("p s w i j -> p w s i j"),
+                    in_=rows.rearrange("p j (w s i) -> p w s i j", s=HALVES, i=PAIR),
+                )
+            out, rows, count = share(u, 2)
+            if count:
+                nc.gpsimd.tensor_scalar(
+                    out=out.rearrange("p s w i j -> p w s i j"),
+                    in0=rows.rearrange("p j (w s i) -> p w s i j", s=HALVES, i=PAIR),
+                    scalar1=1.0,
+                    scalar2=0.0,
+                    op0=mybir.AluOpType.mult,
+                    op1=mybir.AluOpType.add,
+                )
 
         def collect(u):
-            out, rows = share(u, SCALAR_WINDOWS + GPSIMD_WINDOWS, TENSOR_WINDOWS)
+            out, rows, count = share(u, 3)
             nc.scalar.copy(
                 out=out.rearrange("p s w i j -> p s w (i j)"),
                 in_=turned_tiles[u][:].rearrange("p (w s i) j -> p s w (i j)", s=HALVES, i=PAIR),
@@ -209,23 +222,18 @@ def tile_selfattention_pa_t_kernel(tc, x, Wq, Wk, Wv, out_0, out_1, out_2):
                 )
             q_tiles[u] = q_sums
 
-        def result(u):
-            first, size = store_of_unit[u]
-            if first not in result_tiles:
-                q_out = results.tile([P, size * UNIT], F32, tag="q%d" % size)
-                pooled = results.tile([P, POOLED_HEADS, size * UNIT_WINDOWS], F32, tag="pooled%d" % size)
-                result_tiles[first] = (q_out, pooled)
-            return result_tiles[first], u - first
-
         def drain_q(u):
-            (q_out, pooled), at = result(u)
+            first, size = q_piece_of_unit[u]
+            if u == first:
+                q_out_tiles[u] = results.tile([P, size * UNIT], F32, name="q_out", tag="q%d" % size)
+            at = (u - first) * UNIT
             nc.scalar.copy(
-                out=q_out[:, at * UNIT : (at + 1) * UNIT].rearrange("p (w s i) -> p w s i", s=HALVES, i=PAIR),
+                out=q_out_tiles[first][:, at : at + UNIT].rearrange("p (w s i) -> p w s i", s=HALVES, i=PAIR),
                 in_=q_tiles[u][:].rearrange("p s w i -> p w s i"),
             )
-            first, size = store_of_unit[u]
             if u == first + size - 1:
-                store_q(first, size)
+                b, t0 = divmod(first * UNIT, TIME)
+                nc.sync.dma_start(out=out_0[b, :, t0 : t0 + size * UNIT], in_=q_out_tiles[first][:])
 
         def place(g, h, i):
             windows = GROUPS[g] * UNIT_WINDOWS
@@ -237,8 +245,13 @@ def tile_selfattention_pa_t_kernel(tc, x, Wq, Wk, Wv, out_0, out_1, out_2):
         def copy_last_place(g, h):
             windows = GROUPS[g] * UNIT_WINDOWS
             if h == 0:
-                (q_out, pooled), at = result(group_first[g])
-                links = [pooled[:, :, at * UNIT_WINDOWS : at * UNIT_WINDOWS + windows]]
+                first, size = pooled_piece_of_unit[group_first[g]]
+                if first == group_first[g]:
+                    pooled_tiles[first] = results.tile(
+                        [P, POOLED_HEADS, size * UNIT_WINDOWS], F32, name="pooled", tag="pooled%d" % size
+                    )
+                at = (group_first[g] - first) * UNIT_WINDOWS
+                links = [pooled_tiles[first][:, :, at : at + windows]]
                 for i in range(1, WINDOW):
                     link = chain_pool.tile([P, POOLED_HEADS, windows], F32, tag="link%d" % i)
                     links.append(link[:])
@@ -250,23 +263,15 @@ def tile_selfattention_pa_t_kernel(tc, x, Wq, Wk, Wv, out_0, out_1, out_2):
             nc.vector.tensor_tensor(
                 out=links[i][:, h, :], in0=place(g, h, i), in1=links[i + 1][:, h, :], op=mybir.AluOpType.max
             )
-            last = group_first[g] + GROUPS[g] - 1
-            first, size = store_of_unit[last]
-            if i == 0 and h == POOLED_HEADS - 1 and last == first + size - 1:
-                store_pooled(first, size)
+            first, size = pooled_piece_of_unit[group_first[g]]
+            if i == 0 and group_first[g] + GROUPS[g] == first + size:
+                store_pooled(first, size, h)
 
-        def store_q(first, size):
+        def store_pooled(first, size, h):
             b, t0 = divmod(first * UNIT, TIME)
-            nc.sync.dma_start(out=out_0[b, :, t0 : t0 + size * UNIT], in_=result_tiles[first][0][:])
-
-        def store_pooled(first, size):
-            b, t0 = divmod(first * UNIT, TIME)
-            pooled = result_tiles[first][1]
             windows = slice(t0 // WINDOW, (t0 + size * UNIT) // WINDOW)
-            nc.sync.dma_start(out=out_1[b, :, windows], in_=pooled[:, 0, :])
-            nc.sync.dma_start(
-                out=out_2[b, :, windows].rearrange("(h m) w -> m h w", h=2), in_=pooled[:, 1:3, :]
-            )
+            out = out_1[b, :, windows] if h == 0 else out_2[b, (h - 1) * P : h * P, windows]
+            nc.sync.dma_start(out=out, in_=pooled_tiles[first][:, h, :])
 
         w_codes, w_scales = quantise_weights(tc, nc, keep, Wq, Wk, Wv)
         load_after_unit = {}
@@ -299,8 +304,8 @@ def tile_selfattention_pa_t_kernel(tc, x, Wq, Wk, Wv, out_0, out_1, out_2):
             else:
                 copy_last_at[s] = [(g, 0)]
                 copy_first_at[s + 1] = [(g, 1), (g, 2)]
-                links_at.setdefault(s + 1, []).extend(chain[:4])
-                links_at.setdefault(s + 2, []).extend(chain[4:])
+                links_at.setdefault(s + 1, []).extend(chain[:5])
+                links_at.setdefault(s + 2, []).extend(chain[5:])
                 q_at[s + 2] = group_first[g]
                 q_at[s + 3] = group_first[g] + 1
             s += size

@@ -27,14 +27,12 @@ CHUNKS = BATCH * CHUNKS_PER_BATCH
 UNITS = CHUNKS * UNITS_PER_CHUNK
 GROUPS = [1, 1] + [2] * 15
 X_CHUNKS_IN_SBUF = 4
-SHARES = (36, 0, 56, 36)
-FIRST_SHARES = (40, 64, 0, 24)
-FIRST_UNITS = 2
+SHARES = {1: (40, 64, 0, 24), 2: (80, 0, 112, 64)}
 
 FLOPS = 2 * BATCH * TIME * CHANNELS * HEADS * P
 
 assert CHANNELS == P * PACK
-assert sum(SHARES) == sum(FIRST_SHARES) == UNIT_WINDOWS
+assert all(sum(SHARES[size]) == size * UNIT_WINDOWS for size in SHARES)
 assert sum(GROUPS) == UNITS
 
 
@@ -88,13 +86,13 @@ def tile_selfattention_pa_t_kernel(tc, x, Wq, Wk, Wv, out_0, out_1, out_2):
         ctx.enter_context(tc.manual_schedule())
         keep = ctx.enter_context(tc.tile_pool(name="keep", bufs=1))
         x_pool = ctx.enter_context(tc.tile_pool(name="x", bufs=X_CHUNKS_IN_SBUF))
-        grouped_pool = ctx.enter_context(tc.tile_pool(name="grouped", bufs=3))
-        work = ctx.enter_context(tc.tile_pool(name="work", bufs=5))
+        grouped_pool = ctx.enter_context(tc.tile_pool(name="grouped", bufs=2))
+        work = ctx.enter_context(tc.tile_pool(name="work", bufs=3))
         results = ctx.enter_context(tc.tile_pool(name="results", bufs=3))
         chain_pool = ctx.enter_context(tc.tile_pool(name="chain", bufs=2))
         turned_pool = ctx.enter_context(tc.psum_pool(name="turned", bufs=1))
 
-        loads = cut_into_pieces({0: 1, 1: 1, 2: 1, 3: 1, 4: 2, 6: 2})
+        loads = cut_into_pieces({0: 1, 1: 1, 2: 2, 4: 2, 6: 2})
         q_pieces = cut_into_pieces({UNITS - 4: 2, UNITS - 2: 1, UNITS - 1: 1})
         pooled_pieces = cut_into_pieces({UNITS - 4: 2, UNITS - 2: 2})
         q_piece_of_unit = {first + i: (first, size) for first, size in q_pieces for i in range(size)}
@@ -103,7 +101,7 @@ def tile_selfattention_pa_t_kernel(tc, x, Wq, Wk, Wv, out_0, out_1, out_2):
         group_first = [sum(GROUPS[:g]) for g in range(len(GROUPS))]
         group_of_unit = {group_first[g] + i: g for g in range(len(GROUPS)) for i in range(GROUPS[g])}
 
-        x_units = {}
+        x_tiles = {}
         turned_tiles = {}
         grouped_tiles = {}
         codes = {}
@@ -114,24 +112,23 @@ def tile_selfattention_pa_t_kernel(tc, x, Wq, Wk, Wv, out_0, out_1, out_2):
 
         def load(first, size):
             b, t0 = divmod(first * UNIT, TIME)
-            x_rows = x_pool.tile([P, PACK, size * UNIT], BF16, tag="x%d" % size, bufs=2 if size == 2 else X_CHUNKS_IN_SBUF)
+            x_rows = x_pool.tile([P, PACK, size * UNIT], BF16, tag="x%d" % size, bufs={1: 2, 2: 3, 4: X_CHUNKS_IN_SBUF}[size])
             nc.sync.dma_start(
                 out=x_rows[:], in_=x[b, :, t0 : t0 + size * UNIT].rearrange("(p j) t -> p j t", j=PACK)
             )
             for i in range(size):
-                x_units[first + i] = x_rows[:, :, i * UNIT : (i + 1) * UNIT]
+                x_tiles[first + i] = (x_rows, first)
 
-        def share(u, engine):
-            shares = FIRST_SHARES if u < FIRST_UNITS else SHARES
+        def share(g, engine):
+            shares = SHARES[GROUPS[g]]
             first, count = sum(shares[:engine]), shares[engine]
-            g = group_of_unit[u]
-            w0 = (u - group_first[g]) * UNIT_WINDOWS + first
-            out = grouped_tiles[g][:, :, w0 : w0 + count, :, :] if g in grouped_tiles else None
-            return out, x_units[u][:, :, first * WINDOW : (first + count) * WINDOW], count
+            x_rows, x_first = x_tiles[group_first[g]]
+            t0 = (group_first[g] - x_first) * UNIT + first * WINDOW
+            return slice(first, first + count), x_rows[:, :, t0 : t0 + count * WINDOW]
 
-        def turn(u):
-            out, rows, count = share(u, 3)
-            turned = turned_pool.tile([P, count * WINDOW, PACK], BF16)
+        def turn(g):
+            windows, rows = share(g, 3)
+            turned = turned_pool.tile([P, rows.shape[2], PACK], BF16)
             for j in range(0, PACK, 2):
                 nc.tensor.matmul(
                     out=turned[:, :, j : j + 2].rearrange("p t j -> p j t"),
@@ -140,29 +137,26 @@ def tile_selfattention_pa_t_kernel(tc, x, Wq, Wk, Wv, out_0, out_1, out_2):
                     start=True,
                     stop=True,
                 )
-            turned_tiles[u] = turned
+            turned_tiles[g] = turned
 
-        def regroup(u):
-            g = group_of_unit[u]
-            if u == group_first[g]:
-                grouped_tiles[g] = grouped_pool.tile(
-                    [P, HALVES, GROUPS[g] * UNIT_WINDOWS, PAIR, PACK], BF16, name="grouped", align_bytes=64
-                )
-            out, rows, count = share(u, 0)
+        def regroup(g):
+            grouped = grouped_pool.tile([P, HALVES, GROUPS[g] * UNIT_WINDOWS, PAIR, PACK], BF16, align_bytes=64)
+            grouped_tiles[g] = grouped
+            windows, rows = share(g, 0)
             nc.scalar.copy(
-                out=out.rearrange("p s w i j -> p w s j i"),
+                out=grouped[:, :, windows, :, :].rearrange("p s w i j -> p w s j i"),
                 in_=rows.rearrange("p j (w s i) -> p w s j i", s=HALVES, i=PAIR),
             )
-            out, rows, count = share(u, 1)
-            if count:
+            windows, rows = share(g, 1)
+            if GROUPS[g] == 1:
                 nc.vector.tensor_copy(
-                    out=out.rearrange("p s w i j -> p w s i j"),
+                    out=grouped[:, :, windows, :, :].rearrange("p s w i j -> p w s i j"),
                     in_=rows.rearrange("p j (w s i) -> p w s i j", s=HALVES, i=PAIR),
                 )
-            out, rows, count = share(u, 2)
-            if count:
+            else:
+                windows, rows = share(g, 2)
                 nc.gpsimd.tensor_scalar(
-                    out=out.rearrange("p s w i j -> p w s i j"),
+                    out=grouped[:, :, windows, :, :].rearrange("p s w i j -> p w s i j"),
                     in0=rows.rearrange("p j (w s i) -> p w s i j", s=HALVES, i=PAIR),
                     scalar1=1.0,
                     scalar2=0.0,
@@ -170,23 +164,23 @@ def tile_selfattention_pa_t_kernel(tc, x, Wq, Wk, Wv, out_0, out_1, out_2):
                     op1=mybir.AluOpType.add,
                 )
 
-        def collect(u):
-            out, rows, count = share(u, 3)
+        def collect(g):
+            windows, rows = share(g, 3)
             nc.scalar.copy(
-                out=out.rearrange("p s w i j -> p s w (i j)"),
-                in_=turned_tiles[u][:].rearrange("p (w s i) j -> p s w (i j)", s=HALVES, i=PAIR),
+                out=grouped_tiles[g][:, :, windows, :, :].rearrange("p s w i j -> p s w (i j)"),
+                in_=turned_tiles[g][:].rearrange("p (w s i) j -> p s w (i j)", s=HALVES, i=PAIR),
             )
 
-        def quantise(g, part):
-            x_codes = work.tile([P, UNIT], U32, align_bytes=64)
-            x_scales = work.tile([P, UNIT], U8, align_bytes=64)
-            columns = slice(part * UNIT * PACK, (part + 1) * UNIT * PACK)
+        def quantise(g):
+            columns = GROUPS[g] * UNIT
+            x_codes = work.tile([P, columns], U32, align_bytes=64)
+            x_scales = work.tile([P, columns], U8, align_bytes=64)
             nc.vector.quantize_mx(
                 out=x_codes[:].bitcast(FP8X4),
                 scales=x_scales[:],
-                in_=grouped_tiles[g][:].rearrange("p s w i j -> p (s w i j)")[:, columns],
+                in_=grouped_tiles[g][:].rearrange("p s w i j -> p (s w i j)"),
             )
-            codes[(g, part)] = (x_codes, x_scales)
+            codes[g] = (x_codes, x_scales)
 
         def product(out, h, x_codes, x_scales):
             nc.tensor.matmul_mx(
@@ -200,10 +194,11 @@ def tile_selfattention_pa_t_kernel(tc, x, Wq, Wk, Wv, out_0, out_1, out_2):
             )
 
         def multiply(g, part):
-            x_codes, x_scales = codes[(g, part)]
+            x_codes, x_scales = codes[g]
+            columns = slice(part * UNIT, (part + 1) * UNIT)
             for h in range(POOLED_HEADS):
                 sums = psum.tile([P, UNIT], F32, tag="head%d" % h)
-                product(sums[:], h, x_codes[:], x_scales[:])
+                product(sums[:], h, x_codes[:, columns], x_scales[:, columns])
                 sums_tiles[(g, part, h)] = sums
 
         def multiply_q(u):
@@ -211,9 +206,8 @@ def tile_selfattention_pa_t_kernel(tc, x, Wq, Wk, Wv, out_0, out_1, out_2):
             q_sums = psum.tile([P, HALVES, UNIT_WINDOWS, PAIR], F32, tag="q", bufs=1)
             run = UNIT_WINDOWS * PAIR
             for half in range(HALVES):
-                column = (half * GROUPS[g] + u - group_first[g]) * run
-                part, at = divmod(column, UNIT)
-                x_codes, x_scales = codes[(g, part)]
+                at = (half * GROUPS[g] + u - group_first[g]) * run
+                x_codes, x_scales = codes[g]
                 product(
                     q_sums[:, half, :, :].rearrange("p w i -> p (w i)"),
                     Q_HEAD,
@@ -285,54 +279,38 @@ def tile_selfattention_pa_t_kernel(tc, x, Wq, Wk, Wv, out_0, out_1, out_2):
         identity = keep.tile([P, P], BF16)
         make_identity(nc, identity[:])
 
-        regroup_at, quantise_at, copy_first_at, copy_last_at, links_at, q_at = {}, {}, {}, {}, {}, {}
-        heads = list(range(POOLED_HEADS))
-        step = 0
-        for u in range(UNITS):
-            regroup_at.setdefault(step, []).append(u)
-            if u not in (1, 3):
-                step += 1
-        s = 1
-        for g, size in enumerate(GROUPS):
-            for k in range(size):
-                quantise_at[s + k] = (g, size - 1 - k)
-            chain = [(g, i, h) for i in range(WINDOW - 2, -1, -1) for h in heads]
-            if size == 1:
-                copy_first_at[s + 1] = [(g, h) for h in heads]
-                links_at.setdefault(s + 1, []).extend(chain)
-                q_at[s + 1] = group_first[g]
-            else:
-                copy_last_at[s] = [(g, 0)]
-                copy_first_at[s + 1] = [(g, 1), (g, 2)]
-                links_at.setdefault(s + 1, []).extend(chain[:5])
-                links_at.setdefault(s + 2, []).extend(chain[5:])
-                q_at[s + 2] = group_first[g]
-                q_at[s + 3] = group_first[g] + 1
-            s += size
+        def units_of(g):
+            return list(range(group_first[g], group_first[g] + GROUPS[g])) if 0 <= g < len(GROUPS) else []
 
+        heads = range(POOLED_HEADS)
         turn(0)
-        for s in range(UNITS + 4):
-            if s in quantise_at:
-                quantise(*quantise_at[s])
-            for g, h in copy_first_at.get(s, []):
-                copy_last_place(g, h)
-            for u in regroup_at.get(s, []):
-                regroup(u)
+        for g in range(-1, len(GROUPS) + 1):
+            if units_of(g):
+                quantise(g)
+            if units_of(g + 1):
+                regroup(g + 1)
+                collect(g + 1)
+            for u in units_of(g + 1):
                 if u in load_after_unit:
                     load(*load_after_unit[u])
-                collect(u)
-                if u == regroup_at[s][-1]:
-                    break
-                turn(u + 1)
-            if s in q_at:
-                multiply_q(q_at[s])
-            if s in quantise_at:
-                multiply(*quantise_at[s])
-            if s + 1 in regroup_at:
-                turn(regroup_at[s + 1][0])
-            if s in q_at:
-                drain_q(q_at[s])
-            for g, i, h in links_at.get(s, []):
-                link_up(g, i, h)
-            for g, h in copy_last_at.get(s, []):
-                copy_last_place(g, h)
+            q_units = units_of(g - 1)
+            for u in q_units[:1]:
+                multiply_q(u)
+                drain_q(u)
+                for h in heads:
+                    link_up(g - 1, 2, h)
+            if units_of(g):
+                multiply(g, GROUPS[g] - 1)
+            if units_of(g):
+                for h in heads:
+                    copy_last_place(g, h)
+            for u in q_units[1:]:
+                multiply_q(u)
+                drain_q(u)
+            if units_of(g + 2):
+                turn(g + 2)
+            for i in (1, 0) if q_units else ():
+                for h in heads:
+                    link_up(g - 1, i, h)
+            for part in range(GROUPS[g] - 1 if units_of(g) else 0):
+                multiply(g, part)

@@ -20,20 +20,20 @@ POOLED_HEADS = 3
 Q_HEAD = 3
 UNIT = 512
 UNIT_WINDOWS = UNIT // WINDOW
-CHUNK = 2048
-UNITS_PER_CHUNK = CHUNK // UNIT
-CHUNKS_PER_BATCH = TIME // CHUNK
-CHUNKS = BATCH * CHUNKS_PER_BATCH
-UNITS = CHUNKS * UNITS_PER_CHUNK
+UNITS = BATCH * TIME // UNIT
 GROUPS = [1, 1] + [2] * 15
-X_CHUNKS_IN_SBUF = 4
-SHARES = {1: (40, 64, 0, 24), 2: (80, 0, 112, 64)}
+LOADS = [1, 1, 2, 2, 2, 4, 4, 8, 4, 4]
+LOAD_BUFFERS = {1: 2, 2: 3, 4: 2, 8: 1}
+LOAD_AFTER = {8: 11, 9: 15}
+Q_STORES = [4] * 7 + [2, 1, 1]
+POOLED_STORES = [8] * 3 + [4, 2, 2]
+SHARES = [(40, 64, 0, 24)] * 2 + [(96, 32, 64, 64)] + [(96, 0, 96, 64)] + [(88, 0, 104, 64)] * 13
 
 FLOPS = 2 * BATCH * TIME * CHANNELS * HEADS * P
 
 assert CHANNELS == P * PACK
-assert all(sum(SHARES[size]) == size * UNIT_WINDOWS for size in SHARES)
-assert sum(GROUPS) == UNITS
+assert all(sum(share) == size * UNIT_WINDOWS for share, size in zip(SHARES, GROUPS))
+assert sum(GROUPS) == sum(LOADS) == sum(Q_STORES) == sum(POOLED_STORES) == UNITS
 
 
 def quantise_weights(tc, nc, keep, Wq, Wk, Wv):
@@ -72,11 +72,9 @@ def quantise_weights(tc, nc, keep, Wq, Wk, Wv):
 
 
 def cut_into_pieces(sizes):
-    pieces, first = [], 0
-    while first < UNITS:
-        size = sizes.get(first, UNITS_PER_CHUNK)
-        pieces.append((first, size))
-        first += size
+    pieces = []
+    for n, size in enumerate(sizes):
+        pieces.extend([(n, len(pieces), size)] * size)
     return pieces
 
 
@@ -85,19 +83,16 @@ def tile_selfattention_pa_t_kernel(tc, x, Wq, Wk, Wv, out_0, out_1, out_2):
     with ExitStack() as ctx:
         ctx.enter_context(tc.manual_schedule())
         keep = ctx.enter_context(tc.tile_pool(name="keep", bufs=1))
-        x_pool = ctx.enter_context(tc.tile_pool(name="x", bufs=X_CHUNKS_IN_SBUF))
+        x_pool = ctx.enter_context(tc.tile_pool(name="x", bufs=1))
         grouped_pool = ctx.enter_context(tc.tile_pool(name="grouped", bufs=2))
         work = ctx.enter_context(tc.tile_pool(name="work", bufs=3))
-        results = ctx.enter_context(tc.tile_pool(name="results", bufs=3))
+        results = ctx.enter_context(tc.tile_pool(name="results", bufs=1))
         chain_pool = ctx.enter_context(tc.tile_pool(name="chain", bufs=2))
         turned_pool = ctx.enter_context(tc.psum_pool(name="turned", bufs=1))
 
-        loads = cut_into_pieces({0: 1, 1: 1, 2: 2, 4: 2, 6: 2})
-        q_pieces = cut_into_pieces({UNITS - 4: 2, UNITS - 2: 1, UNITS - 1: 1})
-        pooled_pieces = cut_into_pieces({UNITS - 4: 2, UNITS - 2: 2})
-        q_piece_of_unit = {first + i: (first, size) for first, size in q_pieces for i in range(size)}
-        pooled_piece_of_unit = {first + i: (first, size) for first, size in pooled_pieces for i in range(size)}
-
+        load_of_unit = cut_into_pieces(LOADS)
+        q_store_of_unit = cut_into_pieces(Q_STORES)
+        pooled_store_of_unit = cut_into_pieces(POOLED_STORES)
         group_first = [sum(GROUPS[:g]) for g in range(len(GROUPS))]
         group_of_unit = {group_first[g] + i: g for g in range(len(GROUPS)) for i in range(GROUPS[g])}
 
@@ -110,21 +105,20 @@ def tile_selfattention_pa_t_kernel(tc, x, Wq, Wk, Wv, out_0, out_1, out_2):
         q_out_tiles, pooled_tiles = {}, {}
         chains = {}
 
-        def load(first, size):
+        def load(n):
+            first, size = sum(LOADS[:n]), LOADS[n]
             b, t0 = divmod(first * UNIT, TIME)
-            x_rows = x_pool.tile([P, PACK, size * UNIT], BF16, tag="x%d" % size, bufs={1: 2, 2: 3, 4: X_CHUNKS_IN_SBUF}[size])
+            x_rows = x_pool.tile([P, PACK, size * UNIT], BF16, tag="x%d" % size, bufs=LOAD_BUFFERS[size])
             nc.sync.dma_start(
                 out=x_rows[:], in_=x[b, :, t0 : t0 + size * UNIT].rearrange("(p j) t -> p j t", j=PACK)
             )
-            for i in range(size):
-                x_tiles[first + i] = (x_rows, first)
+            x_tiles[n] = x_rows
 
         def share(g, engine):
-            shares = SHARES[GROUPS[g]]
-            first, count = sum(shares[:engine]), shares[engine]
-            x_rows, x_first = x_tiles[group_first[g]]
+            first, count = sum(SHARES[g][:engine]), SHARES[g][engine]
+            n, x_first, size = load_of_unit[group_first[g]]
             t0 = (group_first[g] - x_first) * UNIT + first * WINDOW
-            return slice(first, first + count), x_rows[:, :, t0 : t0 + count * WINDOW]
+            return slice(first, first + count), x_tiles[n][:, :, t0 : t0 + count * WINDOW]
 
         def turn(g):
             windows, rows = share(g, 3)
@@ -148,13 +142,13 @@ def tile_selfattention_pa_t_kernel(tc, x, Wq, Wk, Wv, out_0, out_1, out_2):
                 in_=rows.rearrange("p j (w s i) -> p w s j i", s=HALVES, i=PAIR),
             )
             windows, rows = share(g, 1)
-            if GROUPS[g] == 1:
+            if SHARES[g][1]:
                 nc.vector.tensor_copy(
                     out=grouped[:, :, windows, :, :].rearrange("p s w i j -> p w s i j"),
                     in_=rows.rearrange("p j (w s i) -> p w s i j", s=HALVES, i=PAIR),
                 )
-            else:
-                windows, rows = share(g, 2)
+            windows, rows = share(g, 2)
+            if SHARES[g][2]:
                 nc.gpsimd.tensor_scalar(
                     out=grouped[:, :, windows, :, :].rearrange("p s w i j -> p w s i j"),
                     in0=rows.rearrange("p j (w s i) -> p w s i j", s=HALVES, i=PAIR),
@@ -217,9 +211,9 @@ def tile_selfattention_pa_t_kernel(tc, x, Wq, Wk, Wv, out_0, out_1, out_2):
             q_tiles[u] = q_sums
 
         def drain_q(u):
-            first, size = q_piece_of_unit[u]
+            n, first, size = q_store_of_unit[u]
             if u == first:
-                q_out_tiles[u] = results.tile([P, size * UNIT], F32, name="q_out", tag="q%d" % size)
+                q_out_tiles[u] = results.tile([P, size * UNIT], F32, name="q_out", tag="q%d" % size, bufs=3 if size == 4 else 2)
             at = (u - first) * UNIT
             nc.scalar.copy(
                 out=q_out_tiles[first][:, at : at + UNIT].rearrange("p (w s i) -> p w s i", s=HALVES, i=PAIR),
@@ -239,17 +233,14 @@ def tile_selfattention_pa_t_kernel(tc, x, Wq, Wk, Wv, out_0, out_1, out_2):
         def copy_last_place(g, h):
             windows = GROUPS[g] * UNIT_WINDOWS
             if h == 0:
-                first, size = pooled_piece_of_unit[group_first[g]]
+                n, first, size = pooled_store_of_unit[group_first[g]]
                 if first == group_first[g]:
                     pooled_tiles[first] = results.tile(
-                        [P, POOLED_HEADS, size * UNIT_WINDOWS], F32, name="pooled", tag="pooled%d" % size
+                        [P, POOLED_HEADS, size * UNIT_WINDOWS], F32, name="pooled", tag="pooled%d" % size, bufs=2
                     )
                 at = (group_first[g] - first) * UNIT_WINDOWS
-                links = [pooled_tiles[first][:, :, at : at + windows]]
-                for i in range(1, WINDOW):
-                    link = chain_pool.tile([P, POOLED_HEADS, windows], F32, tag="link%d" % i)
-                    links.append(link[:])
-                chains[g] = links
+                link = chain_pool.tile([P, POOLED_HEADS, windows], F32)
+                chains[g] = [pooled_tiles[first][:, :, at : at + windows]] + [link[:]] * (WINDOW - 1)
             nc.scalar.copy(out=chains[g][WINDOW - 1][:, h, :], in_=place(g, h, WINDOW - 1))
 
         def link_up(g, i, h):
@@ -257,7 +248,7 @@ def tile_selfattention_pa_t_kernel(tc, x, Wq, Wk, Wv, out_0, out_1, out_2):
             nc.vector.tensor_tensor(
                 out=links[i][:, h, :], in0=place(g, h, i), in1=links[i + 1][:, h, :], op=mybir.AluOpType.max
             )
-            first, size = pooled_piece_of_unit[group_first[g]]
+            n, first, size = pooled_store_of_unit[group_first[g]]
             if i == 0 and group_first[g] + GROUPS[g] == first + size:
                 store_pooled(first, size, h)
 
@@ -268,13 +259,10 @@ def tile_selfattention_pa_t_kernel(tc, x, Wq, Wk, Wv, out_0, out_1, out_2):
             nc.sync.dma_start(out=out, in_=pooled_tiles[first][:, h, :])
 
         w_codes, w_scales = quantise_weights(tc, nc, keep, Wq, Wk, Wv)
-        load_after_unit = {}
-        for first, size in loads:
-            after = first - X_CHUNKS_IN_SBUF * UNITS_PER_CHUNK + UNITS_PER_CHUNK - 1
-            if after < 0:
-                load(first, size)
-            else:
-                load_after_unit[after] = (first, size)
+        load_after_unit = {u: n for n, u in LOAD_AFTER.items()}
+        for n in range(len(LOADS)):
+            if n not in LOAD_AFTER:
+                load(n)
         psum = ctx.enter_context(tc.psum_pool(name="sums", bufs=2))
         identity = keep.tile([P, P], BF16)
         make_identity(nc, identity[:])
@@ -292,7 +280,7 @@ def tile_selfattention_pa_t_kernel(tc, x, Wq, Wk, Wv, out_0, out_1, out_2):
                 collect(g + 1)
             for u in units_of(g + 1):
                 if u in load_after_unit:
-                    load(*load_after_unit[u])
+                    load(load_after_unit[u])
             q_units = units_of(g - 1)
             for u in q_units[:1]:
                 multiply_q(u)

@@ -14,8 +14,7 @@ PACK = 4
 BATCH, CHANNELS, TIME = 4, 512, 4096
 WINDOW = 4
 HEADS = 4
-HALVES = 2
-PAIR = WINDOW // HALVES
+PAIR = 2
 POOLED_HEADS = 3
 Q_HEAD = 3
 UNIT = 512
@@ -27,7 +26,7 @@ LOAD_BUFFERS = {1: 2, 2: 3, 4: 2, 8: 1}
 LOAD_AFTER = {8: 11, 9: 15}
 Q_STORES = [4] * 7 + [2, 1, 1]
 POOLED_STORES = [8] * 3 + [4, 2, 2]
-SHARES = [(40, 64, 0, 24)] * 2 + [(96, 32, 64, 64)] + [(96, 0, 96, 64)] + [(88, 0, 104, 64)] * 13
+SHARES = [(40, 64, 0, 24)] * 2 + [(96, 32, 64, 64)] + [(88, 0, 104, 64)] + [(80, 0, 112, 64)] * 13
 
 FLOPS = 2 * BATCH * TIME * CHANNELS * HEADS * P
 
@@ -134,24 +133,24 @@ def tile_selfattention_pa_t_kernel(tc, x, Wq, Wk, Wv, out_0, out_1, out_2):
             turned_tiles[g] = turned
 
         def regroup(g):
-            grouped = grouped_pool.tile([P, HALVES, GROUPS[g] * UNIT_WINDOWS, PAIR, PACK], BF16, align_bytes=64)
+            grouped = grouped_pool.tile([P, WINDOW, GROUPS[g] * UNIT_WINDOWS, PACK], BF16, align_bytes=64)
             grouped_tiles[g] = grouped
             windows, rows = share(g, 0)
             nc.scalar.copy(
-                out=grouped[:, :, windows, :, :].rearrange("p s w i j -> p w s j i"),
-                in_=rows.rearrange("p j (w s i) -> p w s j i", s=HALVES, i=PAIR),
+                out=grouped[:, :, windows, :].rearrange("p i (v w) j -> p v i j w", w=PAIR),
+                in_=rows.rearrange("p j (v w i) -> p v i j w", w=PAIR, i=WINDOW),
             )
             windows, rows = share(g, 1)
             if SHARES[g][1]:
                 nc.vector.tensor_copy(
-                    out=grouped[:, :, windows, :, :].rearrange("p s w i j -> p w s i j"),
-                    in_=rows.rearrange("p j (w s i) -> p w s i j", s=HALVES, i=PAIR),
+                    out=grouped[:, :, windows, :].rearrange("p i w j -> p w i j"),
+                    in_=rows.rearrange("p j (w i) -> p w i j", i=WINDOW),
                 )
             windows, rows = share(g, 2)
             if SHARES[g][2]:
                 nc.gpsimd.tensor_scalar(
-                    out=grouped[:, :, windows, :, :].rearrange("p s w i j -> p w s i j"),
-                    in0=rows.rearrange("p j (w s i) -> p w s i j", s=HALVES, i=PAIR),
+                    out=grouped[:, :, windows, :].rearrange("p i w j -> p w i j"),
+                    in0=rows.rearrange("p j (w i) -> p w i j", i=WINDOW),
                     scalar1=1.0,
                     scalar2=0.0,
                     op0=mybir.AluOpType.mult,
@@ -161,8 +160,8 @@ def tile_selfattention_pa_t_kernel(tc, x, Wq, Wk, Wv, out_0, out_1, out_2):
         def collect(g):
             windows, rows = share(g, 3)
             nc.scalar.copy(
-                out=grouped_tiles[g][:, :, windows, :, :].rearrange("p s w i j -> p s w (i j)"),
-                in_=turned_tiles[g][:].rearrange("p (w s i) j -> p s w (i j)", s=HALVES, i=PAIR),
+                out=grouped_tiles[g][:, :, windows, :],
+                in_=turned_tiles[g][:].rearrange("p (w i) j -> p i w j", i=WINDOW),
             )
 
         def quantise(g):
@@ -172,7 +171,7 @@ def tile_selfattention_pa_t_kernel(tc, x, Wq, Wk, Wv, out_0, out_1, out_2):
             nc.vector.quantize_mx(
                 out=x_codes[:].bitcast(FP8X4),
                 scales=x_scales[:],
-                in_=grouped_tiles[g][:].rearrange("p s w i j -> p (s w i j)"),
+                in_=grouped_tiles[g][:].rearrange("p i w j -> p (i w j)"),
             )
             codes[g] = (x_codes, x_scales)
 
@@ -197,16 +196,12 @@ def tile_selfattention_pa_t_kernel(tc, x, Wq, Wk, Wv, out_0, out_1, out_2):
 
         def multiply_q(u):
             g = group_of_unit[u]
-            q_sums = psum.tile([P, HALVES, UNIT_WINDOWS, PAIR], F32, tag="q", bufs=1)
-            run = UNIT_WINDOWS * PAIR
-            for half in range(HALVES):
-                at = (half * GROUPS[g] + u - group_first[g]) * run
-                x_codes, x_scales = codes[g]
+            q_sums = psum.tile([P, WINDOW, UNIT_WINDOWS], F32, tag="q", bufs=1)
+            x_codes, x_scales = codes[g]
+            for i in range(WINDOW):
+                at = (i * GROUPS[g] + u - group_first[g]) * UNIT_WINDOWS
                 product(
-                    q_sums[:, half, :, :].rearrange("p w i -> p (w i)"),
-                    Q_HEAD,
-                    x_codes[:, at : at + run],
-                    x_scales[:, at : at + run],
+                    q_sums[:, i, :], Q_HEAD, x_codes[:, at : at + UNIT_WINDOWS], x_scales[:, at : at + UNIT_WINDOWS]
                 )
             q_tiles[u] = q_sums
 
@@ -216,8 +211,8 @@ def tile_selfattention_pa_t_kernel(tc, x, Wq, Wk, Wv, out_0, out_1, out_2):
                 q_out_tiles[u] = results.tile([P, size * UNIT], F32, name="q_out", tag="q%d" % size, bufs=3 if size == 4 else 2)
             at = (u - first) * UNIT
             nc.scalar.copy(
-                out=q_out_tiles[first][:, at : at + UNIT].rearrange("p (w s i) -> p w s i", s=HALVES, i=PAIR),
-                in_=q_tiles[u][:].rearrange("p s w i -> p w s i"),
+                out=q_out_tiles[first][:, at : at + UNIT].rearrange("p (w i) -> p w i", i=WINDOW),
+                in_=q_tiles[u][:].rearrange("p i w -> p w i"),
             )
             if u == first + size - 1:
                 b, t0 = divmod(first * UNIT, TIME)
@@ -225,10 +220,8 @@ def tile_selfattention_pa_t_kernel(tc, x, Wq, Wk, Wv, out_0, out_1, out_2):
 
         def place(g, h, i):
             windows = GROUPS[g] * UNIT_WINDOWS
-            half, which = divmod(i, PAIR)
-            part, at = divmod(half * windows * PAIR, UNIT)
-            pairs = sums_tiles[(g, part, h)][:, at : at + windows * PAIR].rearrange("p (w i) -> p i w", i=PAIR)
-            return pairs[:, which, :]
+            part, at = divmod(i * windows, UNIT)
+            return sums_tiles[(g, part, h)][:, at : at + windows]
 
         def copy_last_place(g, h):
             windows = GROUPS[g] * UNIT_WINDOWS

@@ -23,10 +23,10 @@ UNITS = BATCH * TIME // UNIT
 GROUPS = [1, 1] + [2] * 15
 LOADS = [1, 1, 2, 2, 2, 4, 4, 8, 4, 4]
 LOAD_BUFFERS = {1: 2, 2: 3, 4: 2, 8: 1}
-LOAD_AFTER = {8: 11, 9: 15}
+LOAD_AFTER = {7: 9, 8: 13, 9: 17}
 Q_STORES = [4] * 7 + [2, 1, 1]
 POOLED_STORES = [8] * 3 + [4, 2, 2]
-SHARES = [(40, 64, 0, 24)] * 2 + [(96, 32, 64, 64)] + [(88, 0, 104, 64)] + [(80, 0, 112, 64)] * 13
+SHARES = [(32, 48, 24, 24), (56, 40, 0, 32), (80, 64, 48, 64), (88, 16, 88, 64)] + [(80, 12, 108, 56)] * 13
 
 FLOPS = 2 * BATCH * TIME * CHANNELS * HEADS * P
 
@@ -35,24 +35,21 @@ assert all(sum(share) == size * UNIT_WINDOWS for share, size in zip(SHARES, GROU
 assert sum(GROUPS) == sum(LOADS) == sum(Q_STORES) == sum(POOLED_STORES) == UNITS
 
 
-def quantise_weights(tc, nc, keep, Wq, Wk, Wv):
-    with ExitStack() as scope:
-        stage = scope.enter_context(tc.tile_pool(name="w_stage", bufs=1))
-        psum = scope.enter_context(tc.psum_pool(name="w_psum", bufs=2))
+def load_weights(nc, pool, Wq, Wk, Wv):
+    w_rows = pool.tile([P, HEADS, CHANNELS], BF16)
+    nc.sync.dma_start(out=w_rows[:, 0, :], in_=Wk)
+    nc.sync.dma_start(out=w_rows[:, 1:3, :], in_=Wv.rearrange("(h m) c -> m h c", h=2))
+    nc.sync.dma_start(out=w_rows[:, Q_HEAD, :], in_=Wq)
+    return w_rows
 
-        w_rows = stage.tile([P, HEADS, CHANNELS], BF16)
-        nc.sync.dma_start(out=w_rows[:, 0, :], in_=Wk)
-        nc.sync.dma_start(out=w_rows[:, 1:3, :], in_=Wv.rearrange("(h m) c -> m h c", h=2))
-        nc.sync.dma_start(out=w_rows[:, Q_HEAD, :], in_=Wq)
 
-        identity = stage.tile([P, P], F32)
-        make_identity(nc, identity[:])
-
-        w_words = w_rows[:].rearrange("m h c -> m (h c)").bitcast(F32).rearrange(
-            "m (h p e) -> m h e p", h=HEADS, e=2
-        )
-        w_grouped = stage.tile([P, HEADS * P * PACK], BF16, align_bytes=64)
-        w_grouped_words = w_grouped[:].bitcast(F32).rearrange("p (h m e) -> p h m e", h=HEADS, e=2)
+def quantise_weights(tc, nc, pool, w_rows, identity):
+    w_words = w_rows[:].rearrange("m h c -> m (h c)").bitcast(F32).rearrange(
+        "m (h p e) -> m h e p", h=HEADS, e=2
+    )
+    w_grouped = pool.tile([P, HEADS * P * PACK], BF16, align_bytes=64)
+    w_grouped_words = w_grouped[:].bitcast(F32).rearrange("p (h m e) -> p h m e", h=HEADS, e=2)
+    with tc.psum_pool(name="w_psum", bufs=2) as psum:
         for pair in range(HEADS // 2):
             flipped = psum.tile([P, 2, 2, P], F32)
             for i in range(2):
@@ -63,10 +60,9 @@ def quantise_weights(tc, nc, keep, Wq, Wk, Wv):
                 out=w_grouped_words[:, 2 * pair : 2 * pair + 2, :, :],
                 in_=flipped[:].rearrange("p i e m -> p i m e"),
             )
-
-        w_codes = keep.tile([P, HEADS * P], U32, align_bytes=64)
-        w_scales = keep.tile([P, HEADS * P], U8, align_bytes=64)
-        nc.vector.quantize_mx(out=w_codes[:].bitcast(FP8X4), scales=w_scales[:], in_=w_grouped[:])
+    w_codes = pool.tile([P, HEADS * P], U32, align_bytes=64)
+    w_scales = pool.tile([P, HEADS * P], U8, align_bytes=64)
+    nc.vector.quantize_mx(out=w_codes[:].bitcast(FP8X4), scales=w_scales[:], in_=w_grouped[:])
     return w_codes, w_scales
 
 
@@ -251,22 +247,30 @@ def tile_selfattention_pa_t_kernel(tc, x, Wq, Wk, Wv, out_0, out_1, out_2):
             out = out_1[b, :, windows] if h == 0 else out_2[b, (h - 1) * P : h * P, windows]
             nc.sync.dma_start(out=out, in_=pooled_tiles[first][:, h, :])
 
-        w_codes, w_scales = quantise_weights(tc, nc, keep, Wq, Wk, Wv)
         load_after_unit = {u: n for n, u in LOAD_AFTER.items()}
-        for n in range(len(LOADS)):
+        load(0)
+        w_rows = load_weights(nc, keep, Wq, Wk, Wv)
+        for n in range(1, len(LOADS)):
             if n not in LOAD_AFTER:
                 load(n)
-        psum = ctx.enter_context(tc.psum_pool(name="sums", bufs=2))
         identity = keep.tile([P, P], BF16)
         make_identity(nc, identity[:])
+        identity_f32 = keep.tile([P, P], F32)
+        make_identity(nc, identity_f32[:])
 
         def units_of(g):
             return list(range(group_first[g], group_first[g] + GROUPS[g])) if 0 <= g < len(GROUPS) else []
 
         heads = range(POOLED_HEADS)
         turn(0)
-        for g in range(-1, len(GROUPS) + 1):
-            if units_of(g):
+        regroup(0)
+        collect(0)
+        quantise(0)
+        w_codes, w_scales = quantise_weights(tc, nc, keep, w_rows, identity_f32)
+        psum = ctx.enter_context(tc.psum_pool(name="sums", bufs=2))
+        turn(1)
+        for g in range(len(GROUPS) + 1):
+            if g and units_of(g):
                 quantise(g)
             if units_of(g + 1):
                 regroup(g + 1)

@@ -21,12 +21,13 @@ UNIT = 512
 UNIT_WINDOWS = UNIT // WINDOW
 UNITS = BATCH * TIME // UNIT
 GROUPS = [1, 1] + [2] * 15
-LOADS = [1, 1, 2, 2, 2, 4, 4, 8, 4, 4]
-LOAD_BUFFERS = {1: 2, 2: 3, 4: 2, 8: 1}
-LOAD_AFTER = {7: 9, 8: 13, 9: 17}
+LOADS = [1, 1, 2, 2, 2, 4, 4, 4, 4, 2, 2, 2, 2]
+LOAD_BUFFERS = {1: 2, 2: 4, 4: 4}
+LOADS_AT_ONCE = 10
+LOAD_AFTER_GROUP = {2: 10, 3: 11, 4: 12}
 Q_STORES = [4] * 7 + [2, 1, 1]
-POOLED_STORES = [8] * 3 + [4, 2, 2]
-SHARES = [(32, 48, 24, 24), (56, 40, 0, 32), (80, 64, 48, 64), (88, 16, 88, 64)] + [(80, 12, 108, 56)] * 13
+POOLED_STORES = [4] * 7 + [2, 2]
+SHARES = [(32, 48, 24, 24), (56, 40, 0, 32), (80, 64, 48, 64), (88, 16, 88, 64)] + [(80, 8, 108, 60)] * 13
 
 FLOPS = 2 * BATCH * TIME * CHANNELS * HEADS * P
 
@@ -182,10 +183,10 @@ def tile_selfattention_pa_t_kernel(tc, x, Wq, Wk, Wv, out_0, out_1, out_2):
                 stop=True,
             )
 
-        def multiply(g, part):
+        def multiply(g, part, heads):
             x_codes, x_scales = codes[g]
             columns = slice(part * UNIT, (part + 1) * UNIT)
-            for h in range(POOLED_HEADS):
+            for h in heads:
                 sums = psum.tile([P, UNIT], F32, tag="head%d" % h)
                 product(sums[:], h, x_codes[:, columns], x_scales[:, columns])
                 sums_tiles[(g, part, h)] = sums
@@ -204,7 +205,7 @@ def tile_selfattention_pa_t_kernel(tc, x, Wq, Wk, Wv, out_0, out_1, out_2):
         def drain_q(u):
             n, first, size = q_store_of_unit[u]
             if u == first:
-                q_out_tiles[u] = results.tile([P, size * UNIT], F32, name="q_out", tag="q%d" % size, bufs=3 if size == 4 else 2)
+                q_out_tiles[u] = results.tile([P, size * UNIT], F32, name="q_out", tag="q%d" % size, bufs={4: 4, 2: 1, 1: 2}[size])
             at = (u - first) * UNIT
             nc.scalar.copy(
                 out=q_out_tiles[first][:, at : at + UNIT].rearrange("p (w i) -> p w i", i=WINDOW),
@@ -221,11 +222,11 @@ def tile_selfattention_pa_t_kernel(tc, x, Wq, Wk, Wv, out_0, out_1, out_2):
 
         def copy_last_place(g, h):
             windows = GROUPS[g] * UNIT_WINDOWS
-            if h == 0:
+            if g not in chains:
                 n, first, size = pooled_store_of_unit[group_first[g]]
                 if first == group_first[g]:
                     pooled_tiles[first] = results.tile(
-                        [P, POOLED_HEADS, size * UNIT_WINDOWS], F32, name="pooled", tag="pooled%d" % size, bufs=2
+                        [P, POOLED_HEADS, size * UNIT_WINDOWS], F32, name="pooled", tag="pooled%d" % size, bufs=5 if size == 4 else 2
                     )
                 at = (group_first[g] - first) * UNIT_WINDOWS
                 link = chain_pool.tile([P, POOLED_HEADS, windows], F32)
@@ -247,12 +248,10 @@ def tile_selfattention_pa_t_kernel(tc, x, Wq, Wk, Wv, out_0, out_1, out_2):
             out = out_1[b, :, windows] if h == 0 else out_2[b, (h - 1) * P : h * P, windows]
             nc.sync.dma_start(out=out, in_=pooled_tiles[first][:, h, :])
 
-        load_after_unit = {u: n for n, u in LOAD_AFTER.items()}
         load(0)
         w_rows = load_weights(nc, keep, Wq, Wk, Wv)
-        for n in range(1, len(LOADS)):
-            if n not in LOAD_AFTER:
-                load(n)
+        for n in range(1, LOADS_AT_ONCE):
+            load(n)
         identity = keep.tile([P, P], BF16)
         make_identity(nc, identity[:])
         identity_f32 = keep.tile([P, P], F32)
@@ -261,7 +260,6 @@ def tile_selfattention_pa_t_kernel(tc, x, Wq, Wk, Wv, out_0, out_1, out_2):
         def units_of(g):
             return list(range(group_first[g], group_first[g] + GROUPS[g])) if 0 <= g < len(GROUPS) else []
 
-        heads = range(POOLED_HEADS)
         turn(0)
         regroup(0)
         collect(0)
@@ -275,27 +273,28 @@ def tile_selfattention_pa_t_kernel(tc, x, Wq, Wk, Wv, out_0, out_1, out_2):
             if units_of(g + 1):
                 regroup(g + 1)
                 collect(g + 1)
-            for u in units_of(g + 1):
-                if u in load_after_unit:
-                    load(load_after_unit[u])
+            if g + 1 in LOAD_AFTER_GROUP:
+                load(LOAD_AFTER_GROUP[g + 1])
             q_units = units_of(g - 1)
             for u in q_units[:1]:
                 multiply_q(u)
                 drain_q(u)
-                for h in heads:
+                for h in (0, 1, 2):
                     link_up(g - 1, 2, h)
             if units_of(g):
-                multiply(g, GROUPS[g] - 1)
+                multiply(g, GROUPS[g] - 1, (0, 1, 2))
             if units_of(g):
-                for h in heads:
+                for h in (0, 1, 2):
                     copy_last_place(g, h)
             for u in q_units[1:]:
                 multiply_q(u)
                 drain_q(u)
             if units_of(g + 2):
                 turn(g + 2)
-            for i in (1, 0) if q_units else ():
-                for h in heads:
-                    link_up(g - 1, i, h)
+            if q_units:
+                for h in (0, 1, 2):
+                    link_up(g - 1, 1, h)
+                for h in (1, 2, 0):
+                    link_up(g - 1, 0, h)
             for part in range(GROUPS[g] - 1 if units_of(g) else 0):
-                multiply(g, part)
+                multiply(g, part, (1, 2, 0))

from contextlib import ExitStack

import concourse.mybir as mybir
from concourse.masks import make_identity

BF16 = mybir.dt.bfloat16
F32 = mybir.dt.float32
U32 = mybir.dt.uint32
U8 = mybir.dt.uint8
FP8X4 = mybir.dt.float8_e4m3fn_x4

P = 128
PACK = 4
BATCH, CHANNELS, TIME = 4, 512, 4096
WINDOW = 4
HEADS = 4
PAIR = 2
POOLED_HEADS = 3
Q_HEAD = 3
UNIT = 512
UNIT_WINDOWS = UNIT // WINDOW
UNITS = BATCH * TIME // UNIT
GROUPS = [1, 1] + [2] * 15
LOADS = [1, 1, 2, 2, 2, 4, 4, 4, 4, 2, 2, 2, 2]
LOAD_BUFFERS = {1: 2, 2: 4, 4: 4}
LOADS_AT_ONCE = 10
LOAD_AFTER_GROUP = {2: 10, 3: 11, 4: 12}
Q_STORES = [4] * 7 + [2, 1, 1]
POOLED_STORES = [4] * 7 + [2, 2]
SHARES = [(32, 48, 24, 24), (56, 40, 0, 32), (80, 64, 48, 64), (88, 16, 88, 64)] + [(80, 8, 108, 60)] * 13

FLOPS = 2 * BATCH * TIME * CHANNELS * HEADS * P

assert CHANNELS == P * PACK
assert all(sum(share) == size * UNIT_WINDOWS for share, size in zip(SHARES, GROUPS))
assert sum(GROUPS) == sum(LOADS) == sum(Q_STORES) == sum(POOLED_STORES) == UNITS


def load_weights(nc, pool, Wq, Wk, Wv):
    w_rows = pool.tile([P, HEADS, CHANNELS], BF16)
    nc.sync.dma_start(out=w_rows[:, 0, :], in_=Wk)
    nc.sync.dma_start(out=w_rows[:, 1:3, :], in_=Wv.rearrange("(h m) c -> m h c", h=2))
    nc.sync.dma_start(out=w_rows[:, Q_HEAD, :], in_=Wq)
    return w_rows


def quantise_weights(tc, nc, pool, w_rows, identity):
    w_words = w_rows[:].rearrange("m h c -> m (h c)").bitcast(F32).rearrange(
        "m (h p e) -> m h e p", h=HEADS, e=2
    )
    w_grouped = pool.tile([P, HEADS * P * PACK], BF16, align_bytes=64)
    w_grouped_words = w_grouped[:].bitcast(F32).rearrange("p (h m e) -> p h m e", h=HEADS, e=2)
    with tc.psum_pool(name="w_psum", bufs=2) as psum:
        for pair in range(HEADS // 2):
            flipped = psum.tile([P, 2, 2, P], F32)
            for i in range(2):
                for e in range(2):
                    nc.tensor.transpose(flipped[:, i, e, :], w_words[:, 2 * pair + i, e, :], identity[:])
            copy = nc.scalar.copy if pair == 0 else nc.vector.tensor_copy
            copy(
                out=w_grouped_words[:, 2 * pair : 2 * pair + 2, :, :],
                in_=flipped[:].rearrange("p i e m -> p i m e"),
            )
    w_codes = pool.tile([P, HEADS * P], U32, align_bytes=64)
    w_scales = pool.tile([P, HEADS * P], U8, align_bytes=64)
    nc.vector.quantize_mx(out=w_codes[:].bitcast(FP8X4), scales=w_scales[:], in_=w_grouped[:])
    return w_codes, w_scales


def cut_into_pieces(sizes):
    pieces = []
    for n, size in enumerate(sizes):
        pieces.extend([(n, len(pieces), size)] * size)
    return pieces


def tile_selfattention_pa_t_kernel(tc, x, Wq, Wk, Wv, out_0, out_1, out_2):
    nc = tc.nc
    with ExitStack() as ctx:
        ctx.enter_context(tc.manual_schedule())
        keep = ctx.enter_context(tc.tile_pool(name="keep", bufs=1))
        x_pool = ctx.enter_context(tc.tile_pool(name="x", bufs=1))
        grouped_pool = ctx.enter_context(tc.tile_pool(name="grouped", bufs=2))
        work = ctx.enter_context(tc.tile_pool(name="work", bufs=3))
        results = ctx.enter_context(tc.tile_pool(name="results", bufs=1))
        chain_pool = ctx.enter_context(tc.tile_pool(name="chain", bufs=2))
        turned_pool = ctx.enter_context(tc.psum_pool(name="turned", bufs=1))

        load_of_unit = cut_into_pieces(LOADS)
        q_store_of_unit = cut_into_pieces(Q_STORES)
        pooled_store_of_unit = cut_into_pieces(POOLED_STORES)
        group_first = [sum(GROUPS[:g]) for g in range(len(GROUPS))]
        group_of_unit = {group_first[g] + i: g for g in range(len(GROUPS)) for i in range(GROUPS[g])}

        x_tiles = {}
        turned_tiles = {}
        grouped_tiles = {}
        codes = {}
        sums_tiles = {}
        q_tiles = {}
        q_out_tiles, pooled_tiles = {}, {}
        chains = {}

        def load(n):
            first, size = sum(LOADS[:n]), LOADS[n]
            b, t0 = divmod(first * UNIT, TIME)
            x_rows = x_pool.tile([P, PACK, size * UNIT], BF16, tag="x%d" % size, bufs=LOAD_BUFFERS[size])
            nc.sync.dma_start(
                out=x_rows[:], in_=x[b, :, t0 : t0 + size * UNIT].rearrange("(p j) t -> p j t", j=PACK)
            )
            x_tiles[n] = x_rows

        def share(g, engine):
            first, count = sum(SHARES[g][:engine]), SHARES[g][engine]
            n, x_first, size = load_of_unit[group_first[g]]
            t0 = (group_first[g] - x_first) * UNIT + first * WINDOW
            return slice(first, first + count), x_tiles[n][:, :, t0 : t0 + count * WINDOW]

        def turn(g):
            windows, rows = share(g, 3)
            turned = turned_pool.tile([P, rows.shape[2], PACK], BF16)
            for j in range(0, PACK, 2):
                nc.tensor.matmul(
                    out=turned[:, :, j : j + 2].rearrange("p t j -> p j t"),
                    lhsT=identity[:],
                    rhs=rows[:, j : j + 2, :],
                    start=True,
                    stop=True,
                )
            turned_tiles[g] = turned

        def regroup(g):
            grouped = grouped_pool.tile([P, WINDOW, GROUPS[g] * UNIT_WINDOWS, PACK], BF16, align_bytes=64)
            grouped_tiles[g] = grouped
            windows, rows = share(g, 0)
            nc.scalar.copy(
                out=grouped[:, :, windows, :].rearrange("p i (v w) j -> p v i j w", w=PAIR),
                in_=rows.rearrange("p j (v w i) -> p v i j w", w=PAIR, i=WINDOW),
            )
            windows, rows = share(g, 1)
            if SHARES[g][1]:
                nc.vector.tensor_copy(
                    out=grouped[:, :, windows, :].rearrange("p i w j -> p w i j"),
                    in_=rows.rearrange("p j (w i) -> p w i j", i=WINDOW),
                )
            windows, rows = share(g, 2)
            if SHARES[g][2]:
                nc.gpsimd.tensor_scalar(
                    out=grouped[:, :, windows, :].rearrange("p i w j -> p w i j"),
                    in0=rows.rearrange("p j (w i) -> p w i j", i=WINDOW),
                    scalar1=1.0,
                    scalar2=0.0,
                    op0=mybir.AluOpType.mult,
                    op1=mybir.AluOpType.add,
                )

        def collect(g):
            windows, rows = share(g, 3)
            nc.scalar.copy(
                out=grouped_tiles[g][:, :, windows, :],
                in_=turned_tiles[g][:].rearrange("p (w i) j -> p i w j", i=WINDOW),
            )

        def quantise(g):
            columns = GROUPS[g] * UNIT
            x_codes = work.tile([P, columns], U32, align_bytes=64)
            x_scales = work.tile([P, columns], U8, align_bytes=64)
            nc.vector.quantize_mx(
                out=x_codes[:].bitcast(FP8X4),
                scales=x_scales[:],
                in_=grouped_tiles[g][:].rearrange("p i w j -> p (i w j)"),
            )
            codes[g] = (x_codes, x_scales)

        def product(out, h, x_codes, x_scales):
            nc.tensor.matmul_mx(
                out=out,
                lhsT=w_codes[:, h * P : (h + 1) * P].bitcast(FP8X4),
                lhsT_scale=w_scales[:, h * P : (h + 1) * P],
                rhs=x_codes.bitcast(FP8X4),
                rhs_scale=x_scales,
                start=True,
                stop=True,
            )

        def multiply(g, part, heads):
            x_codes, x_scales = codes[g]
            columns = slice(part * UNIT, (part + 1) * UNIT)
            for h in heads:
                sums = psum.tile([P, UNIT], F32, tag="head%d" % h)
                product(sums[:], h, x_codes[:, columns], x_scales[:, columns])
                sums_tiles[(g, part, h)] = sums

        def multiply_q(u):
            g = group_of_unit[u]
            q_sums = psum.tile([P, WINDOW, UNIT_WINDOWS], F32, tag="q", bufs=1)
            x_codes, x_scales = codes[g]
            for i in range(WINDOW):
                at = (i * GROUPS[g] + u - group_first[g]) * UNIT_WINDOWS
                product(
                    q_sums[:, i, :], Q_HEAD, x_codes[:, at : at + UNIT_WINDOWS], x_scales[:, at : at + UNIT_WINDOWS]
                )
            q_tiles[u] = q_sums

        def drain_q(u):
            n, first, size = q_store_of_unit[u]
            if u == first:
                q_out_tiles[u] = results.tile([P, size * UNIT], F32, name="q_out", tag="q%d" % size, bufs={4: 4, 2: 1, 1: 2}[size])
            at = (u - first) * UNIT
            nc.scalar.copy(
                out=q_out_tiles[first][:, at : at + UNIT].rearrange("p (w i) -> p w i", i=WINDOW),
                in_=q_tiles[u][:].rearrange("p i w -> p w i"),
            )
            if u == first + size - 1:
                b, t0 = divmod(first * UNIT, TIME)
                nc.sync.dma_start(out=out_0[b, :, t0 : t0 + size * UNIT], in_=q_out_tiles[first][:])

        def place(g, h, i):
            windows = GROUPS[g] * UNIT_WINDOWS
            part, at = divmod(i * windows, UNIT)
            return sums_tiles[(g, part, h)][:, at : at + windows]

        def copy_last_place(g, h):
            windows = GROUPS[g] * UNIT_WINDOWS
            if g not in chains:
                n, first, size = pooled_store_of_unit[group_first[g]]
                if first == group_first[g]:
                    pooled_tiles[first] = results.tile(
                        [P, POOLED_HEADS, size * UNIT_WINDOWS], F32, name="pooled", tag="pooled%d" % size, bufs=5 if size == 4 else 2
                    )
                at = (group_first[g] - first) * UNIT_WINDOWS
                link = chain_pool.tile([P, POOLED_HEADS, windows], F32)
                chains[g] = [pooled_tiles[first][:, :, at : at + windows]] + [link[:]] * (WINDOW - 1)
            nc.scalar.copy(out=chains[g][WINDOW - 1][:, h, :], in_=place(g, h, WINDOW - 1))

        def link_up(g, i, h):
            links = chains[g]
            nc.vector.tensor_tensor(
                out=links[i][:, h, :], in0=place(g, h, i), in1=links[i + 1][:, h, :], op=mybir.AluOpType.max
            )
            n, first, size = pooled_store_of_unit[group_first[g]]
            if i == 0 and group_first[g] + GROUPS[g] == first + size:
                store_pooled(first, size, h)

        def store_pooled(first, size, h):
            b, t0 = divmod(first * UNIT, TIME)
            windows = slice(t0 // WINDOW, (t0 + size * UNIT) // WINDOW)
            out = out_1[b, :, windows] if h == 0 else out_2[b, (h - 1) * P : h * P, windows]
            nc.sync.dma_start(out=out, in_=pooled_tiles[first][:, h, :])

        load(0)
        w_rows = load_weights(nc, keep, Wq, Wk, Wv)
        for n in range(1, LOADS_AT_ONCE):
            load(n)
        identity = keep.tile([P, P], BF16)
        make_identity(nc, identity[:])
        identity_f32 = keep.tile([P, P], F32)
        make_identity(nc, identity_f32[:])

        def units_of(g):
            return list(range(group_first[g], group_first[g] + GROUPS[g])) if 0 <= g < len(GROUPS) else []

        turn(0)
        regroup(0)
        collect(0)
        quantise(0)
        w_codes, w_scales = quantise_weights(tc, nc, keep, w_rows, identity_f32)
        psum = ctx.enter_context(tc.psum_pool(name="sums", bufs=2))
        turn(1)
        for g in range(len(GROUPS) + 1):
            if g and units_of(g):
                quantise(g)
            if units_of(g + 1):
                regroup(g + 1)
                collect(g + 1)
            if g + 1 in LOAD_AFTER_GROUP:
                load(LOAD_AFTER_GROUP[g + 1])
            q_units = units_of(g - 1)
            for u in q_units[:1]:
                multiply_q(u)
                drain_q(u)
                for h in (0, 1, 2):
                    link_up(g - 1, 2, h)
            if units_of(g):
                multiply(g, GROUPS[g] - 1, (0, 1, 2))
            if units_of(g):
                for h in (0, 1, 2):
                    copy_last_place(g, h)
            for u in q_units[1:]:
                multiply_q(u)
                drain_q(u)
            if units_of(g + 2):
                turn(g + 2)
            if q_units:
                for h in (0, 1, 2):
                    link_up(g - 1, 1, h)
                for h in (1, 2, 0):
                    link_up(g - 1, 0, h)
            for part in range(GROUPS[g] - 1 if units_of(g) else 0):
                multiply(g, part, (1, 2, 0))
